import numpy as np
import ml_dtypes


def mxq(x, axis, fmt="e4m3"):
    dtype, down = {"e4m3": (ml_dtypes.float8_e4m3fn, 7), "e5m2": (ml_dtypes.float8_e5m2, 14)}[fmt]
    v = np.moveaxis(np.asarray(x, np.float32).astype(ml_dtypes.bfloat16).astype(np.float64), axis, -1)
    blocks = v.reshape(v.shape[:-1] + (-1, 32))
    amax = np.abs(blocks).max(-1, keepdims=True)
    byte = np.maximum(np.where(amax > 0, np.frexp(amax)[1] - 1 + 127, 0) - down, 1)
    scale = np.exp2(byte - 127.0)
    codes = (blocks / scale).astype(np.float32).astype(dtype).astype(np.float64)
    return np.moveaxis((codes * scale).reshape(v.shape), -1, axis)


WIDE = False


def mx_kscale(k):
    if not WIDE:
        return np.ones(k)
    levels = np.array([10, -10, 5, -5, 0])
    if k % 512:
        return np.exp2(np.random.permutation(np.resize(levels, k // 32))).repeat(32)
    a = np.empty((k // 512, 16))
    for p in range(k // 512):
        a[p, :8] = np.random.permutation(np.resize(levels, 8))
        for g in range(8):
            far = levels[np.abs(levels - a[p, g]) >= 10]
            a[p, g + 8] = far[np.random.randint(len(far))]
    return np.exp2(a.ravel()).repeat(32)


BF16 = ml_dtypes.bfloat16


def bf(x):
    return np.asarray(x, np.float32).astype(BF16)


def f64(x):
    return np.asarray(x).astype(np.float64)


M, N, E, P, S, B, KT = 1024, 512, 16, 32, 17, 128, 2


def setup_inputs():
    s = mx_kscale(N)
    eye = np.concatenate([np.eye(N), np.zeros((N, M - N))], axis=1)
    return {
        "context": bf(np.random.standard_normal((S, B, N)) * s),
        "D": bf((eye + np.random.standard_normal((N, M)) * 0.3 / np.sqrt(M)) * s[:, None]),
        "z": bf(np.random.standard_normal((M, B))),
        "conv_w": bf(np.random.standard_normal((N, N, KT)) / np.sqrt(N) / s[None, :, None]),
        "conv_b": bf(np.random.standard_normal(N) * 0.1),
        "t1": bf(np.sqrt(np.sum(s * s)) * (0.5 + 0.1 * np.random.random_sample(1))),
    }


def reference(context, D, z, conv_w, conv_b, t1):
    c = f64(context)
    z_obs = f64(D) @ f64(z)
    distances = np.sum(np.abs(c[:-1] - z_obs.T[None, :, :]), axis=2)
    lg = -distances / f64(t1)[0]
    ex = np.exp(lg - lg.max(axis=0, keepdims=True))
    attn = ex / ex.sum(axis=0, keepdims=True)
    cq = mxq(c, 2, "e4m3")
    w = f64(conv_w)
    encoded = ((cq[:-1] @ mxq(w[:, :, 0], 1, "e4m3").T)
               + (cq[1:] @ mxq(w[:, :, 1], 1, "e4m3").T)
               + f64(conv_b))
    return np.sum(encoded * attn[:, :, None], axis=0)

@@ -1,0 +1,285 @@
+from contextlib import ExitStack
+
+import concourse.mybir as mybir
+from concourse.masks import make_identity
+
+F32 = mybir.dt.float32
+BF16 = mybir.dt.bfloat16
+U32 = mybir.dt.uint32
+U8 = mybir.dt.uint8
+FP8X4 = mybir.dt.float8_e4m3fn_x4
+ALU = mybir.AluOpType
+ACT = mybir.ActivationFunctionType
+AX = mybir.AxisListType
+
+P = 128
+FRAMES = 16
+LOADED = FRAMES + 1
+CH = 512
+LATENT = 1024
+PAIRS = LOADED // 2
+PSUM_BANKS = 8
+FLOPS = 2 * FRAMES * P * CH * CH * 2 + 2 * CH * LATENT * P
+
+GPSIMD_PAIRS = (6, 7)
+SCALAR_FRAMES = (1, 4, 7, 10, 13)
+VECTOR_FRAMES = tuple(s for s in range(FRAMES) if s not in SCALAR_FRAMES)
+BANK_STEPS = (
+    (("C", 0), ("C", 1)),
+    (("W", 0), ("C", 2)),
+    (("W", 1), ("C", 3)),
+    (("W", 2), ("C", 4)),
+    (("W", 3), ("C", 5)),
+    (("C", 6), ("C", 7)),
+    (("C", 8),),
+)
+AHEAD = 2
+
+
+def tile_dynamix_pa_kernel(tc, context, D, z, conv_w, conv_b, t1, out):
+    nc = tc.nc
+    with ExitStack() as stack:
+        keep = stack.enter_context(tc.tile_pool(name="keep", bufs=1))
+        psum = stack.enter_context(tc.psum_pool(name="psum", bufs=PSUM_BANKS))
+        stack.enter_context(tc.manual_schedule())
+
+        ident = keep.tile([P, P], F32)
+        make_identity(nc, ident[:])
+
+        d_sb = keep.tile([P, 4, LATENT], BF16)
+        z_sb = keep.tile([P, 4, 2, P], BF16)
+        t1_bf = keep.tile([P, 1], BF16)
+        c_sb = keep.tile([P, LOADED, CH], BF16)
+        w_sb = keep.tile([P, 4, 2 * CH], BF16)
+        bias_bc = keep.tile([P, CH], BF16)
+
+        def load_d(c):
+            nc.sync.dma_start(out=d_sb[:, c, :], in_=D[c * P:(c + 1) * P, :])
+
+        def load_frames(g):
+            s0, s1 = 2 * g, min(2 * g + 2, LOADED)
+            nc.sync.dma_start(out=c_sb[:, s0:s1, :], in_=context[s0:s1].rearrange("s b i -> b s i"))
+
+        load_d(0)
+        load_d(1)
+        nc.sync.dma_start(out=z_sb[:], in_=z.rearrange("(u q e) b -> q u e b", u=4, e=2))
+        load_d(2)
+        load_d(3)
+        nc.sync.dma_start(out=t1_bf[:], in_=t1.partition_broadcast(P))
+        load_frames(0)
+        load_frames(1)
+        for c in range(4):
+            nc.sync.dma_start(out=w_sb[:, c, :], in_=conv_w[c * P:(c + 1) * P].rearrange("o i t -> o (i t)"))
+        for g in range(2, PAIRS + 1):
+            load_frames(g)
+        nc.sync.dma_start(out=bias_bc[:], in_=conv_b.partition_broadcast(P))
+
+        bank = {}
+
+        def new_bank(key, name):
+            bank[key] = psum.tile([P, CH], F32, tag="bank", name=name)
+            return bank[key]
+
+        d_t = keep.tile([P, 4 * CH], F32)
+        d_t_words = d_t[:].rearrange("q (u i) -> q u i", u=4)
+        d_t_halves = d_t[:].bitcast(BF16).rearrange("q (u i e) -> q u i e", u=4, e=2)
+
+        def transpose_d(c):
+            words = d_sb[:, c, :].bitcast(F32)
+            for h in range(2):
+                target = new_bank(("D", c, h), "d%d%d" % (c, h))
+                for v in range(2):
+                    u = 2 * h + v
+                    nc.tensor.transpose(target[:, v * P:(v + 1) * P], words[:, u * P:(u + 1) * P], ident[:])
+
+        def copy_d(c):
+            cols = slice(c * P, (c + 1) * P)
+            nc.vector.tensor_copy(
+                out=d_t_words[:, 0:2, cols], in_=bank["D", c, 0][:, 0:2 * P].rearrange("q (u i) -> q u i", u=2)
+            )
+            nc.scalar.copy(
+                out=d_t_words[:, 2:4, cols], in_=bank["D", c, 1][:, 0:2 * P].rearrange("q (u i) -> q u i", u=2)
+            )
+
+        def z_obs_columns(c):
+            cols = slice(c * P, (c + 1) * P)
+            for k in range(8):
+                nc.tensor.matmul(
+                    bank["Z"][:, cols],
+                    lhsT=z_sb[:, k // 2, k % 2, :],
+                    rhs=d_t_halves[:, k // 2, cols, k % 2],
+                    start=(k == 0),
+                    stop=(k == 7),
+                )
+
+        for c in range(4):
+            transpose_d(c)
+            copy_d(c)
+            if c == 1:
+                new_bank("Z", "z_obs")
+            if c > 0:
+                z_obs_columns(c - 1)
+        z_obs_columns(3)
+
+        w_taps = keep.tile([P, 4, 2, CH], BF16)
+        for c in range(4):
+            nc.gpsimd.tensor_scalar(
+                out=w_taps[:, c, :, :],
+                in0=w_sb[:, c, :].rearrange("o (i t) -> o t i", t=2),
+                scalar1=1.0,
+                scalar2=0.0,
+                op0=ALU.mult,
+                op1=ALU.add,
+            )
+
+        c_grouped = keep.tile([P, LOADED * CH], BF16, align_bytes=64)
+        c_codes = keep.tile([P, LOADED * P], U32, align_bytes=64)
+        c_scales = keep.tile([P, LOADED * P], U8, align_bytes=64)
+        w_grouped = keep.tile([P, 2, 4 * CH], BF16, align_bytes=64)
+        w_codes = keep.tile([P, 2, CH], U32, align_bytes=64)
+        w_scales = keep.tile([P, 2, CH], U8, align_bytes=64)
+        w_grouped_words = (
+            w_grouped[:].rearrange("q t k -> q (t k)").bitcast(F32).rearrange("q (t o u) -> q t o u", t=2, u=2)
+        )
+
+        def frames_of(g):
+            return min(2, LOADED - 2 * g)
+
+        def transpose_bank(kind, j):
+            target = new_bank((kind, j), "%s%d" % (kind, j))
+            for v in range(4 if kind == "W" else 2 * frames_of(j)):
+                row = w_taps[:, j, v // 2, :] if kind == "W" else c_sb[:, 2 * j + v // 2, :]
+                u = v % 2
+                nc.tensor.transpose(target[:, v * P:(v + 1) * P], row.bitcast(F32)[:, u::2], ident[:])
+
+        def empty_bank(kind, j, on_scalar):
+            if kind == "W":
+                dst = w_grouped_words[:, :, j * P:(j + 1) * P, :]
+                src = bank[kind, j][:].rearrange("q (t u o) -> q t o u", t=2, u=2)
+            else:
+                n = frames_of(j)
+                dst = c_grouped[:, 2 * j * CH:(2 * j + n) * CH].bitcast(F32).rearrange(
+                    "q (s b u) -> q s b u", s=n, u=2
+                )
+                src = bank[kind, j][:, 0:2 * n * P].rearrange("q (s u b) -> q s b u", s=n, u=2)
+            if on_scalar:
+                nc.scalar.copy(out=dst, in_=src)
+            else:
+                nc.vector.tensor_copy(out=dst, in_=src)
+
+        z_obs_sb = keep.tile([P, CH], F32)
+        diff = keep.tile([P, FRAMES, CH], F32)
+        dist = keep.tile([P, FRAMES], F32)
+        unused = keep.tile([P, CH], BF16)
+        inv_t1 = keep.tile([P, 1], F32)
+
+        for step in BANK_STEPS[0:AHEAD]:
+            for kind, j in step:
+                transpose_bank(kind, j)
+        for k in range(PAIRS):
+            step = BANK_STEPS[k] if k < len(BANK_STEPS) else ()
+            if len(step) > 0:
+                empty_bank(step[0][0], step[0][1], True)
+            if k not in GPSIMD_PAIRS:
+                nc.vector.tensor_tensor(
+                    out=diff[:, 2 * k:2 * k + 2, :],
+                    in0=c_sb[:, 2 * k:2 * k + 2, :],
+                    in1=bank["Z"][:].unsqueeze(1).to_broadcast([P, 2, CH]),
+                    op=ALU.subtract,
+                )
+            for s in (2 * k, 2 * k + 1):
+                nc.scalar.activation(out=unused[:], in_=diff[:, s, :], func=ACT.Abs, accum_out=dist[:, s:s + 1])
+            if len(step) > 1:
+                empty_bank(step[1][0], step[1][1], False)
+            if k == 1:
+                nc.vector.tensor_copy(out=z_obs_sb[:], in_=bank["Z"][:])
+                nc.vector.reciprocal(out=inv_t1[:], in_=t1_bf[:])
+                for g in GPSIMD_PAIRS:
+                    for s in (2 * g, 2 * g + 1):
+                        nc.gpsimd.tensor_tensor(
+                            out=diff[:, s, :], in0=c_sb[:, s, :], in1=z_obs_sb[:], op=ALU.subtract
+                        )
+            if k + AHEAD < len(BANK_STEPS):
+                for kind, j in BANK_STEPS[k + AHEAD]:
+                    transpose_bank(kind, j)
+
+        def enc_frame(s):
+            target = new_bank(("X", s), "enc%d" % s)
+            for t in range(2):
+                nc.tensor.matmul_mx(
+                    out=target[:],
+                    lhsT=c_codes[:, (s + t) * P:(s + t + 1) * P].bitcast(FP8X4),
+                    lhsT_scale=c_scales[:, (s + t) * P:(s + t + 1) * P],
+                    rhs=w_codes[:, t, :].bitcast(FP8X4),
+                    rhs_scale=w_scales[:, t, :],
+                    start=(t == 0),
+                    stop=(t == 1),
+                )
+
+        for t in range(2):
+            nc.vector.quantize_mx(
+                out=w_codes[:, t, :].bitcast(FP8X4), scales=w_scales[:, t, :], in_=w_grouped[:, t, :]
+            )
+        started = 0
+        for s0 in range(0, LOADED, 4):
+            s1 = min(s0 + 4, LOADED)
+            nc.vector.quantize_mx(
+                out=c_codes[:, s0 * P:s1 * P].bitcast(FP8X4),
+                scales=c_scales[:, s0 * P:s1 * P],
+                in_=c_grouped[:, s0 * CH:s1 * CH],
+            )
+            ready = min(s1 - 1, PSUM_BANKS)
+            for s in range(started, ready):
+                enc_frame(s)
+            started = ready
+
+        least = keep.tile([P, 1], F32)
+        logit = keep.tile([P, FRAMES], F32)
+        expd = keep.tile([P, FRAMES], F32)
+        total = keep.tile([P, 1], F32)
+        inv_total = keep.tile([P, 1], F32)
+        attn = keep.tile([P, FRAMES], F32)
+        nc.vector.tensor_reduce(out=least[:], in_=dist[:], axis=AX.X, op=ALU.min)
+        nc.vector.tensor_scalar(
+            out=logit[:], in0=dist[:], scalar1=least[:], scalar2=inv_t1[:], op0=ALU.subtract, op1=ALU.mult
+        )
+        nc.scalar.activation(out=expd[:], in_=logit[:], func=ACT.Exp, scale=-1.0, accum_out=total[:])
+        nc.vector.reciprocal(out=inv_total[:], in_=total[:])
+        nc.vector.tensor_scalar(out=attn[:], in0=expd[:], scalar1=inv_total[:], scalar2=None, op0=ALU.mult)
+
+        sums = (keep.tile([P, CH], F32, name="sum_even"), keep.tile([P, CH], F32, name="sum_odd"))
+        sum_gpsimd = keep.tile([P, CH], F32)
+        weighted = keep.tile([P, len(SCALAR_FRAMES), CH], F32)
+        result = keep.tile([P, CH], F32)
+        for s in range(FRAMES):
+            enc = bank["X", s]
+            weight = attn[:, s:s + 1]
+            if s in SCALAR_FRAMES:
+                k = SCALAR_FRAMES.index(s)
+                nc.scalar.activation(out=weighted[:, k, :], in_=enc[:], func=ACT.Copy, scale=weight)
+                if k > 0:
+                    nc.gpsimd.tensor_tensor(
+                        out=sum_gpsimd[:],
+                        in0=(weighted[:, 0, :] if k == 1 else sum_gpsimd[:]),
+                        in1=weighted[:, k, :],
+                        op=ALU.add,
+                    )
+            else:
+                k = VECTOR_FRAMES.index(s)
+                acc = sums[k % 2]
+                if k == 1:
+                    nc.vector.tensor_scalar(out=acc[:], in0=enc[:], scalar1=weight, scalar2=None, op0=ALU.mult)
+                else:
+                    nc.vector.scalar_tensor_tensor(
+                        out=acc[:],
+                        in0=enc[:],
+                        scalar=weight,
+                        in1=(bias_bc[:] if k == 0 else acc[:]),
+                        op0=ALU.mult,
+                        op1=ALU.add,
+                    )
+            if s + PSUM_BANKS < FRAMES:
+                enc_frame(s + PSUM_BANKS)
+        nc.vector.tensor_tensor(out=sums[0][:], in0=sums[0][:], in1=sums[1][:], op=ALU.add)
+        nc.vector.tensor_tensor(out=result[:], in0=sums[0][:], in1=sum_gpsimd[:], op=ALU.add)
+        nc.sync.dma_start(out=out[:, :], in_=result[:])

@@ -21,30 +21,29 @@ PAIRS = LOADED // 2
 PSUM_BANKS = 8
 FLOPS = 2 * FRAMES * P * CH * CH * 2 + 2 * CH * LATENT * P
 
-GPSIMD_PAIRS = (6, 7)
+MAX_FRAMES = 12
 SCALAR_FRAMES = (1, 4, 7, 10, 13)
 VECTOR_FRAMES = tuple(s for s in range(FRAMES) if s not in SCALAR_FRAMES)
-BANK_STEPS = (
-    (("C", 0), ("C", 1)),
-    (("W", 0), ("C", 2)),
-    (("W", 1), ("C", 3)),
-    (("W", 2), ("C", 4)),
-    (("W", 3), ("C", 5)),
-    (("C", 6), ("C", 7)),
-    (("C", 8),),
+ORDER = (
+    ("C", 0), ("C", 1), ("W", 0), ("C", 2), ("W", 1), ("C", 3), ("W", 2), ("C", 4), ("W", 3), ("C", 5),
+    ("C", 6), ("C", 7), ("C", 8),
 )
-AHEAD = 2
+ROTATING = 6
+SUM_BANK = 6
+Z_BANK = 7
 
 
 def tile_dynamix_pa_kernel(tc, context, D, z, conv_w, conv_b, t1, out):
     nc = tc.nc
     with ExitStack() as stack:
         keep = stack.enter_context(tc.tile_pool(name="keep", bufs=1))
-        psum = stack.enter_context(tc.psum_pool(name="psum", bufs=PSUM_BANKS))
+        psum = stack.enter_context(tc.psum_pool(name="psum", bufs=1))
         stack.enter_context(tc.manual_schedule())
 
         ident = keep.tile([P, P], F32)
         make_identity(nc, ident[:])
+        ones = keep.tile([P, 1], BF16)
+        nc.vector.memset(ones[:], 1.0)
 
         d_sb = keep.tile([P, 4, LATENT], BF16)
         z_sb = keep.tile([P, 4, 2, P], BF16)
@@ -76,8 +75,8 @@ def tile_dynamix_pa_kernel(tc, context, D, z, conv_w, conv_b, t1, out):
 
         bank = {}
 
-        def new_bank(key, name):
-            bank[key] = psum.tile([P, CH], F32, tag="bank", name=name)
+        def new_bank(key, name, number):
+            bank[key] = psum.tile([P, CH], F32, tag="bank%d" % number, name=name)
             return bank[key]
 
         d_t = keep.tile([P, 4 * CH], F32)
@@ -87,7 +86,7 @@ def tile_dynamix_pa_kernel(tc, context, D, z, conv_w, conv_b, t1, out):
         def transpose_d(c):
             words = d_sb[:, c, :].bitcast(F32)
             for h in range(2):
-                target = new_bank(("D", c, h), "d%d%d" % (c, h))
+                target = new_bank(("D", c, h), "d%d%d" % (c, h), (2 * c + h) % ROTATING)
                 for v in range(2):
                     u = 2 * h + v
                     nc.tensor.transpose(target[:, v * P:(v + 1) * P], words[:, u * P:(u + 1) * P], ident[:])
@@ -112,11 +111,10 @@ def tile_dynamix_pa_kernel(tc, context, D, z, conv_w, conv_b, t1, out):
                     stop=(k == 7),
                 )
 
+        new_bank("Z", "z_obs", Z_BANK)
         for c in range(4):
             transpose_d(c)
             copy_d(c)
-            if c == 1:
-                new_bank("Z", "z_obs")
             if c > 0:
                 z_obs_columns(c - 1)
         z_obs_columns(3)
@@ -141,70 +139,102 @@ def tile_dynamix_pa_kernel(tc, context, D, z, conv_w, conv_b, t1, out):
         w_grouped_words = (
             w_grouped[:].rearrange("q t k -> q (t k)").bitcast(F32).rearrange("q (t o u) -> q t o u", t=2, u=2)
         )
+        c_by_place = c_grouped[:].rearrange("q (s b k) -> q s b k", s=LOADED, k=4)
 
         def frames_of(g):
             return min(2, LOADED - 2 * g)
 
-        def transpose_bank(kind, j):
-            target = new_bank((kind, j), "%s%d" % (kind, j))
+        def transpose_bank(n):
+            kind, j = ORDER[n]
+            target = new_bank((kind, j), "%s%d" % (kind, j), (n + 2) % ROTATING)
             for v in range(4 if kind == "W" else 2 * frames_of(j)):
                 row = w_taps[:, j, v // 2, :] if kind == "W" else c_sb[:, 2 * j + v // 2, :]
                 u = v % 2
                 nc.tensor.transpose(target[:, v * P:(v + 1) * P], row.bitcast(F32)[:, u::2], ident[:])
 
-        def empty_bank(kind, j, on_scalar):
+        def empty_bank(n):
+            kind, j = ORDER[n]
             if kind == "W":
                 dst = w_grouped_words[:, :, j * P:(j + 1) * P, :]
                 src = bank[kind, j][:].rearrange("q (t u o) -> q t o u", t=2, u=2)
             else:
-                n = frames_of(j)
-                dst = c_grouped[:, 2 * j * CH:(2 * j + n) * CH].bitcast(F32).rearrange(
-                    "q (s b u) -> q s b u", s=n, u=2
+                f = frames_of(j)
+                dst = c_grouped[:, 2 * j * CH:(2 * j + f) * CH].bitcast(F32).rearrange(
+                    "q (s b u) -> q s b u", s=f, u=2
                 )
-                src = bank[kind, j][:, 0:2 * n * P].rearrange("q (s u b) -> q s b u", s=n, u=2)
-            if on_scalar:
-                nc.scalar.copy(out=dst, in_=src)
-            else:
-                nc.vector.tensor_copy(out=dst, in_=src)
+                src = bank[kind, j][:, 0:2 * f * P].rearrange("q (s u b) -> q s b u", s=f, u=2)
+            nc.scalar.copy(out=dst, in_=src)
 
         z_obs_sb = keep.tile([P, CH], F32)
-        diff = keep.tile([P, FRAMES, CH], F32)
+        diff = keep.tile([P, FRAMES - MAX_FRAMES, CH], F32)
+        max_sum = keep.tile([P, MAX_FRAMES], F32)
+        z_sum = keep.tile([P, 1], F32)
+        linear = keep.tile([P, MAX_FRAMES], F32)
         dist = keep.tile([P, FRAMES], F32)
-        unused = keep.tile([P, CH], BF16)
+        unused = keep.tile([P, FRAMES, CH], BF16)
         inv_t1 = keep.tile([P, 1], F32)
 
-        for step in BANK_STEPS[0:AHEAD]:
-            for kind, j in step:
-                transpose_bank(kind, j)
-        for k in range(PAIRS):
-            step = BANK_STEPS[k] if k < len(BANK_STEPS) else ()
-            if len(step) > 0:
-                empty_bank(step[0][0], step[0][1], True)
-            if k not in GPSIMD_PAIRS:
-                nc.vector.tensor_tensor(
-                    out=diff[:, 2 * k:2 * k + 2, :],
-                    in0=c_sb[:, 2 * k:2 * k + 2, :],
-                    in1=bank["Z"][:].unsqueeze(1).to_broadcast([P, 2, CH]),
-                    op=ALU.subtract,
+        def max_frame(s):
+            nc.vector.scalar_tensor_tensor(
+                out=unused[:, s, :], in0=c_sb[:, s, :], scalar=1.0, in1=bank["Z"][:], op0=ALU.mult, op1=ALU.max,
+                accum_out=max_sum[:, s:s + 1],
+            )
+
+        def abs_frame(s):
+            nc.scalar.activation(out=unused[:, s, :], in_=diff[:, s - MAX_FRAMES, :], func=ACT.Abs,
+                                 accum_out=dist[:, s:s + 1])
+
+        def sum_frame(s):
+            for k in range(4):
+                nc.tensor.matmul(
+                    bank["S"][:, s:s + 1], lhsT=c_by_place[:, s, :, k], rhs=ones[:], start=(k == 0), stop=(k == 3)
                 )
-            for s in (2 * k, 2 * k + 1):
-                nc.scalar.activation(out=unused[:], in_=diff[:, s, :], func=ACT.Abs, accum_out=dist[:, s:s + 1])
-            if len(step) > 1:
-                empty_bank(step[1][0], step[1][1], False)
-            if k == 1:
-                nc.vector.tensor_copy(out=z_obs_sb[:], in_=bank["Z"][:])
+
+        def quantize_w(t):
+            nc.vector.quantize_mx(
+                out=w_codes[:, t, :].bitcast(FP8X4), scales=w_scales[:, t, :], in_=w_grouped[:, t, :]
+            )
+
+        def quantize_c(s0):
+            s1 = min(s0 + 4, LOADED)
+            nc.vector.quantize_mx(
+                out=c_codes[:, s0 * P:s1 * P].bitcast(FP8X4),
+                scales=c_scales[:, s0 * P:s1 * P],
+                in_=c_grouped[:, s0 * CH:s1 * CH],
+            )
+
+        new_bank("S", "c_sums", SUM_BANK)
+        for n in range(ROTATING - 2):
+            transpose_bank(n)
+        max_frame(0)
+        max_frame(1)
+        for n in range(len(ORDER)):
+            empty_bank(n)
+            kind, j = ORDER[n]
+            if kind == "C" and 2 * j < MAX_FRAMES:
+                sum_frame(2 * j)
+                sum_frame(2 * j + 1)
+            if n + ROTATING - 2 < len(ORDER):
+                transpose_bank(n + ROTATING - 2)
+            if n == 2:
+                nc.scalar.activation(out=z_obs_sb[:], in_=bank["Z"][:], func=ACT.Copy, accum_out=z_sum[:])
+                for s in range(MAX_FRAMES, FRAMES):
+                    nc.gpsimd.tensor_tensor(
+                        out=diff[:, s - MAX_FRAMES, :], in0=c_sb[:, s, :], in1=z_obs_sb[:], op=ALU.subtract
+                    )
                 nc.vector.reciprocal(out=inv_t1[:], in_=t1_bf[:])
-                for g in GPSIMD_PAIRS:
-                    for s in (2 * g, 2 * g + 1):
-                        nc.gpsimd.tensor_tensor(
-                            out=diff[:, s, :], in0=c_sb[:, s, :], in1=z_obs_sb[:], op=ALU.subtract
-                        )
-            if k + AHEAD < len(BANK_STEPS):
-                for kind, j in BANK_STEPS[k + AHEAD]:
-                    transpose_bank(kind, j)
+                quantize_c(0)
+            elif n >= 10:
+                abs_frame(n + 2)
+            if n + 2 < MAX_FRAMES:
+                max_frame(n + 2)
+        abs_frame(15)
+
+        def enc_bank(s):
+            return (len(ORDER) + 2 + s) % ROTATING if s < ROTATING else s
 
         def enc_frame(s):
-            target = new_bank(("X", s), "enc%d" % s)
+            target = new_bank(("X", s), "enc%d" % s, enc_bank(s % PSUM_BANKS))
             for t in range(2):
                 nc.tensor.matmul_mx(
                     out=target[:],
@@ -216,22 +246,18 @@ def tile_dynamix_pa_kernel(tc, context, D, z, conv_w, conv_b, t1, out):
                     stop=(t == 1),
                 )
 
-        for t in range(2):
-            nc.vector.quantize_mx(
-                out=w_codes[:, t, :].bitcast(FP8X4), scales=w_scales[:, t, :], in_=w_grouped[:, t, :]
-            )
-        started = 0
-        for s0 in range(0, LOADED, 4):
-            s1 = min(s0 + 4, LOADED)
-            nc.vector.quantize_mx(
-                out=c_codes[:, s0 * P:s1 * P].bitcast(FP8X4),
-                scales=c_scales[:, s0 * P:s1 * P],
-                in_=c_grouped[:, s0 * CH:s1 * CH],
-            )
-            ready = min(s1 - 1, PSUM_BANKS)
-            for s in range(started, ready):
-                enc_frame(s)
-            started = ready
+        quantize_w(0)
+        quantize_w(1)
+        nc.vector.tensor_scalar(
+            out=linear[:], in0=bank["S"][:, 0:MAX_FRAMES], scalar1=z_sum[:], scalar2=None, op0=ALU.add
+        )
+        quantize_c(4)
+        nc.vector.scalar_tensor_tensor(
+            out=dist[:, 0:MAX_FRAMES], in0=max_sum[:], scalar=2.0, in1=linear[:], op0=ALU.mult, op1=ALU.subtract
+        )
+        quantize_c(8)
+        for s in range(PSUM_BANKS):
+            enc_frame(s)
 
         least = keep.tile([P, 1], F32)
         logit = keep.tile([P, FRAMES], F32)
@@ -244,6 +270,8 @@ def tile_dynamix_pa_kernel(tc, context, D, z, conv_w, conv_b, t1, out):
             out=logit[:], in0=dist[:], scalar1=least[:], scalar2=inv_t1[:], op0=ALU.subtract, op1=ALU.mult
         )
         nc.scalar.activation(out=expd[:], in_=logit[:], func=ACT.Exp, scale=-1.0, accum_out=total[:])
+        quantize_c(12)
+        quantize_c(16)
         nc.vector.reciprocal(out=inv_total[:], in_=total[:])
         nc.vector.tensor_scalar(out=attn[:], in0=expd[:], scalar1=inv_total[:], scalar2=None, op0=ALU.mult)
 

@@ -64,13 +64,13 @@ def tile_dynamix_pa_kernel(tc, context, D, z, conv_w, conv_b, t1, out):
         nc.sync.dma_start(out=z_sb[:], in_=z.rearrange("(u q e) b -> q u e b", u=4, e=2))
         load_d(2)
         load_d(3)
-        nc.sync.dma_start(out=t1_bf[:], in_=t1.partition_broadcast(P))
         load_frames(0)
         load_frames(1)
         for c in range(4):
             nc.sync.dma_start(out=w_sb[:, c, :], in_=conv_w[c * P:(c + 1) * P].rearrange("o i t -> o (i t)"))
         for g in range(2, PAIRS + 1):
             load_frames(g)
+        nc.sync.dma_start(out=t1_bf[:], in_=t1.partition_broadcast(P))
         nc.sync.dma_start(out=bias_bc[:], in_=conv_b.partition_broadcast(P))
 
         bank = {}
@@ -222,7 +222,6 @@ def tile_dynamix_pa_kernel(tc, context, D, z, conv_w, conv_b, t1, out):
                     nc.gpsimd.tensor_tensor(
                         out=diff[:, s - MAX_FRAMES, :], in0=c_sb[:, s, :], in1=z_obs_sb[:], op=ALU.subtract
                     )
-                nc.vector.reciprocal(out=inv_t1[:], in_=t1_bf[:])
                 quantize_c(0)
             elif n >= 10:
                 abs_frame(n + 2)
@@ -248,6 +247,7 @@ def tile_dynamix_pa_kernel(tc, context, D, z, conv_w, conv_b, t1, out):
 
         quantize_w(0)
         quantize_w(1)
+        nc.vector.reciprocal(out=inv_t1[:], in_=t1_bf[:])
         nc.vector.tensor_scalar(
             out=linear[:], in0=bank["S"][:, 0:MAX_FRAMES], scalar1=z_sum[:], scalar2=None, op0=ALU.add
         )

@@ -21,13 +21,16 @@ PAIRS = LOADED // 2
 PSUM_BANKS = 8
 FLOPS = 2 * FRAMES * P * CH * CH * 2 + 2 * CH * LATENT * P
 
-MAX_FRAMES = 12
+MAX_FRAMES = 10
+LOAD_ORDER = (5, 0, 1, 6, 2, 3, 7, 4, 8)
 SCALAR_FRAMES = (1, 4, 7, 10, 13)
 VECTOR_FRAMES = tuple(s for s in range(FRAMES) if s not in SCALAR_FRAMES)
 ORDER = (
-    ("C", 0), ("C", 1), ("W", 0), ("C", 2), ("W", 1), ("C", 3), ("W", 2), ("C", 4), ("W", 3), ("C", 5),
+    ("W", 0), ("W", 1), ("W", 2), ("W", 3), ("C", 0), ("C", 1), ("C", 2), ("C", 3), ("C", 4), ("C", 5),
     ("C", 6), ("C", 7), ("C", 8),
 )
+VECTOR_EMPTIES = (10, 12)
+WARM_UPS = 3
 ROTATING = 6
 SUM_BANK = 6
 Z_BANK = 7
@@ -64,11 +67,9 @@ def tile_dynamix_pa_kernel(tc, context, D, z, conv_w, conv_b, t1, out):
         nc.sync.dma_start(out=z_sb[:], in_=z.rearrange("(u q e) b -> q u e b", u=4, e=2))
         load_d(2)
         load_d(3)
-        load_frames(0)
-        load_frames(1)
         for c in range(4):
             nc.sync.dma_start(out=w_sb[:, c, :], in_=conv_w[c * P:(c + 1) * P].rearrange("o i t -> o (i t)"))
-        for g in range(2, PAIRS + 1):
+        for g in LOAD_ORDER:
             load_frames(g)
         nc.sync.dma_start(out=t1_bf[:], in_=t1.partition_broadcast(P))
         nc.sync.dma_start(out=bias_bc[:], in_=conv_b.partition_broadcast(P))
@@ -100,8 +101,8 @@ def tile_dynamix_pa_kernel(tc, context, D, z, conv_w, conv_b, t1, out):
                 out=d_t_words[:, 2:4, cols], in_=bank["D", c, 1][:, 0:2 * P].rearrange("q (u i) -> q u i", u=2)
             )
 
-        def z_obs_columns(c):
-            cols = slice(c * P, (c + 1) * P)
+        def z_obs_half(h):
+            cols = slice(2 * h * P, 2 * (h + 1) * P)
             for k in range(8):
                 nc.tensor.matmul(
                     bank["Z"][:, cols],
@@ -111,24 +112,38 @@ def tile_dynamix_pa_kernel(tc, context, D, z, conv_w, conv_b, t1, out):
                     stop=(k == 7),
                 )
 
-        new_bank("Z", "z_obs", Z_BANK)
-        for c in range(4):
-            transpose_d(c)
-            copy_d(c)
-            if c > 0:
-                z_obs_columns(c - 1)
-        z_obs_columns(3)
+        w_taps = keep.tile([P, 4, 2, 2, 2 * P], BF16)
 
-        w_taps = keep.tile([P, 4, 2, CH], BF16)
+        def part_taps(c):
+            for t in range(2):
+                nc.vector.tensor_copy(
+                    out=w_taps[:, c, t, :, :].rearrange("o u (q e) -> o u q e", e=2),
+                    in_=w_sb[:, c, :].rearrange("o (q u e t) -> o t u q e", u=2, e=2, t=2)[:, t],
+                )
+
+        new_bank("Z", "z_obs", Z_BANK)
+        zeros = keep.tile([P, P], F32)
+        nc.vector.memset(zeros[:], 0.0)
+        new_bank("warm", "warm", ROTATING - 1)
+
+        def warm_up():
+            nc.tensor.matmul(bank["warm"][:, 0:P], lhsT=zeros[:], rhs=zeros[:], start=True, stop=True)
+
+        for i in range(WARM_UPS):
+            warm_up()
+        transpose_d(0)
+        copy_d(0)
+        transpose_d(1)
+        copy_d(1)
+        warm_up()
+        z_obs_half(0)
+        transpose_d(2)
+        copy_d(2)
+        transpose_d(3)
+        copy_d(3)
+        z_obs_half(1)
         for c in range(4):
-            nc.gpsimd.tensor_scalar(
-                out=w_taps[:, c, :, :],
-                in0=w_sb[:, c, :].rearrange("o (i t) -> o t i", t=2),
-                scalar1=1.0,
-                scalar2=0.0,
-                op0=ALU.mult,
-                op1=ALU.add,
-            )
+            part_taps(c)
 
         c_grouped = keep.tile([P, LOADED * CH], BF16, align_bytes=64)
         c_codes = keep.tile([P, LOADED * P], U32, align_bytes=64)
@@ -148,9 +163,12 @@ def tile_dynamix_pa_kernel(tc, context, D, z, conv_w, conv_b, t1, out):
             kind, j = ORDER[n]
             target = new_bank((kind, j), "%s%d" % (kind, j), (n + 2) % ROTATING)
             for v in range(4 if kind == "W" else 2 * frames_of(j)):
-                row = w_taps[:, j, v // 2, :] if kind == "W" else c_sb[:, 2 * j + v // 2, :]
                 u = v % 2
-                nc.tensor.transpose(target[:, v * P:(v + 1) * P], row.bitcast(F32)[:, u::2], ident[:])
+                if kind == "W":
+                    words = w_taps[:, j, v // 2, u, :].bitcast(F32)
+                else:
+                    words = c_sb[:, 2 * j + v // 2, :].bitcast(F32)[:, u::2]
+                nc.tensor.transpose(target[:, v * P:(v + 1) * P], words, ident[:])
 
         def empty_bank(n):
             kind, j = ORDER[n]
@@ -163,7 +181,10 @@ def tile_dynamix_pa_kernel(tc, context, D, z, conv_w, conv_b, t1, out):
                     "q (s b u) -> q s b u", s=f, u=2
                 )
                 src = bank[kind, j][:, 0:2 * f * P].rearrange("q (s u b) -> q s b u", s=f, u=2)
-            nc.scalar.copy(out=dst, in_=src)
+            if n in VECTOR_EMPTIES:
+                nc.vector.tensor_copy(out=dst, in_=src)
+            else:
+                nc.scalar.copy(out=dst, in_=src)
 
         z_obs_sb = keep.tile([P, CH], F32)
         diff = keep.tile([P, FRAMES - MAX_FRAMES, CH], F32)
@@ -204,11 +225,17 @@ def tile_dynamix_pa_kernel(tc, context, D, z, conv_w, conv_b, t1, out):
             )
 
         new_bank("S", "c_sums", SUM_BANK)
+        nc.scalar.activation(out=z_obs_sb[:], in_=bank["Z"][:], func=ACT.Copy, accum_out=z_sum[:])
+        for s in range(MAX_FRAMES, FRAMES):
+            nc.gpsimd.tensor_tensor(
+                out=diff[:, s - MAX_FRAMES, :], in0=c_sb[:, s, :], in1=z_obs_sb[:], op=ALU.subtract
+            )
         for n in range(ROTATING - 2):
             transpose_bank(n)
-        max_frame(0)
-        max_frame(1)
         for n in range(len(ORDER)):
+            if n == 10:
+                quantize_c(0)
+                quantize_c(4)
             empty_bank(n)
             kind, j = ORDER[n]
             if kind == "C" and 2 * j < MAX_FRAMES:
@@ -216,18 +243,13 @@ def tile_dynamix_pa_kernel(tc, context, D, z, conv_w, conv_b, t1, out):
                 sum_frame(2 * j + 1)
             if n + ROTATING - 2 < len(ORDER):
                 transpose_bank(n + ROTATING - 2)
-            if n == 2:
-                nc.scalar.activation(out=z_obs_sb[:], in_=bank["Z"][:], func=ACT.Copy, accum_out=z_sum[:])
-                for s in range(MAX_FRAMES, FRAMES):
-                    nc.gpsimd.tensor_tensor(
-                        out=diff[:, s - MAX_FRAMES, :], in0=c_sb[:, s, :], in1=z_obs_sb[:], op=ALU.subtract
-                    )
-                quantize_c(0)
-            elif n >= 10:
-                abs_frame(n + 2)
-            if n + 2 < MAX_FRAMES:
-                max_frame(n + 2)
-        abs_frame(15)
+            if 4 <= n < 4 + FRAMES - MAX_FRAMES:
+                abs_frame(MAX_FRAMES + n - 4)
+            if n < MAX_FRAMES:
+                max_frame(n)
+            if n == 6:
+                quantize_w(0)
+                quantize_w(1)
 
         def enc_bank(s):
             return (len(ORDER) + 2 + s) % ROTATING if s < ROTATING else s
@@ -245,13 +267,10 @@ def tile_dynamix_pa_kernel(tc, context, D, z, conv_w, conv_b, t1, out):
                     stop=(t == 1),
                 )
 
-        quantize_w(0)
-        quantize_w(1)
         nc.vector.reciprocal(out=inv_t1[:], in_=t1_bf[:])
         nc.vector.tensor_scalar(
             out=linear[:], in0=bank["S"][:, 0:MAX_FRAMES], scalar1=z_sum[:], scalar2=None, op0=ALU.add
         )
-        quantize_c(4)
         nc.vector.scalar_tensor_tensor(
             out=dist[:, 0:MAX_FRAMES], in0=max_sum[:], scalar=2.0, in1=linear[:], op0=ALU.mult, op1=ALU.subtract
         )

@@ -23,13 +23,12 @@ FLOPS = 2 * FRAMES * P * CH * CH * 2 + 2 * CH * LATENT * P
 
 MAX_FRAMES = 10
 LOAD_ORDER = (5, 0, 1, 6, 2, 3, 7, 4, 8)
-SCALAR_FRAMES = (1, 4, 7, 10, 13)
+SCALAR_FRAMES = (1, 3, 5, 7, 9)
 VECTOR_FRAMES = tuple(s for s in range(FRAMES) if s not in SCALAR_FRAMES)
 ORDER = (
     ("W", 0), ("W", 1), ("W", 2), ("W", 3), ("C", 0), ("C", 1), ("C", 2), ("C", 3), ("C", 4), ("C", 5),
     ("C", 6), ("C", 7), ("C", 8),
 )
-VECTOR_EMPTIES = (10, 12)
 WARM_UPS = 3
 ROTATING = 6
 SUM_BANK = 6
@@ -101,9 +100,9 @@ def tile_dynamix_pa_kernel(tc, context, D, z, conv_w, conv_b, t1, out):
                 out=d_t_words[:, 2:4, cols], in_=bank["D", c, 1][:, 0:2 * P].rearrange("q (u i) -> q u i", u=2)
             )
 
-        def z_obs_half(h):
+        def z_obs_half(h, k0, k1):
             cols = slice(2 * h * P, 2 * (h + 1) * P)
-            for k in range(8):
+            for k in range(k0, k1):
                 nc.tensor.matmul(
                     bank["Z"][:, cols],
                     lhsT=z_sb[:, k // 2, k % 2, :],
@@ -136,12 +135,13 @@ def tile_dynamix_pa_kernel(tc, context, D, z, conv_w, conv_b, t1, out):
         transpose_d(1)
         copy_d(1)
         warm_up()
-        z_obs_half(0)
         transpose_d(2)
         copy_d(2)
+        z_obs_half(0, 0, 4)
         transpose_d(3)
         copy_d(3)
-        z_obs_half(1)
+        z_obs_half(0, 4, 8)
+        z_obs_half(1, 0, 8)
         for c in range(4):
             part_taps(c)
 
@@ -181,10 +181,7 @@ def tile_dynamix_pa_kernel(tc, context, D, z, conv_w, conv_b, t1, out):
                     "q (s b u) -> q s b u", s=f, u=2
                 )
                 src = bank[kind, j][:, 0:2 * f * P].rearrange("q (s u b) -> q s b u", s=f, u=2)
-            if n in VECTOR_EMPTIES:
-                nc.vector.tensor_copy(out=dst, in_=src)
-            else:
-                nc.scalar.copy(out=dst, in_=src)
+            nc.scalar.copy(out=dst, in_=src)
 
         z_obs_sb = keep.tile([P, CH], F32)
         diff = keep.tile([P, FRAMES - MAX_FRAMES, CH], F32)
@@ -225,17 +222,14 @@ def tile_dynamix_pa_kernel(tc, context, D, z, conv_w, conv_b, t1, out):
             )
 
         new_bank("S", "c_sums", SUM_BANK)
-        nc.scalar.activation(out=z_obs_sb[:], in_=bank["Z"][:], func=ACT.Copy, accum_out=z_sum[:])
+        nc.vector.tensor_copy(out=z_obs_sb[:], in_=bank["Z"][:])
         for s in range(MAX_FRAMES, FRAMES):
             nc.gpsimd.tensor_tensor(
                 out=diff[:, s - MAX_FRAMES, :], in0=c_sb[:, s, :], in1=z_obs_sb[:], op=ALU.subtract
             )
         for n in range(ROTATING - 2):
             transpose_bank(n)
-        for n in range(len(ORDER)):
-            if n == 10:
-                quantize_c(0)
-                quantize_c(4)
+        for n in range(len(ORDER) - 3):
             empty_bank(n)
             kind, j = ORDER[n]
             if kind == "C" and 2 * j < MAX_FRAMES:
@@ -243,19 +237,18 @@ def tile_dynamix_pa_kernel(tc, context, D, z, conv_w, conv_b, t1, out):
                 sum_frame(2 * j + 1)
             if n + ROTATING - 2 < len(ORDER):
                 transpose_bank(n + ROTATING - 2)
+            if n == 8:
+                nc.scalar.activation(out=unused[:, 0, :], in_=z_obs_sb[:], func=ACT.Copy, accum_out=z_sum[:])
             if 4 <= n < 4 + FRAMES - MAX_FRAMES:
                 abs_frame(MAX_FRAMES + n - 4)
             if n < MAX_FRAMES:
                 max_frame(n)
-            if n == 6:
-                quantize_w(0)
-                quantize_w(1)
+        empty_bank(len(ORDER) - 3)
 
-        def enc_bank(s):
-            return (len(ORDER) + 2 + s) % ROTATING if s < ROTATING else s
+        ENC_BANKS = (3, 4, 6, 7, 5, 0, 1, 2)
 
         def enc_frame(s):
-            target = new_bank(("X", s), "enc%d" % s, enc_bank(s % PSUM_BANKS))
+            target = new_bank(("X", s), "enc%d" % s, ENC_BANKS[s % PSUM_BANKS])
             for t in range(2):
                 nc.tensor.matmul_mx(
                     out=target[:],
@@ -267,66 +260,74 @@ def tile_dynamix_pa_kernel(tc, context, D, z, conv_w, conv_b, t1, out):
                     stop=(t == 1),
                 )
 
-        nc.vector.reciprocal(out=inv_t1[:], in_=t1_bf[:])
-        nc.vector.tensor_scalar(
-            out=linear[:], in0=bank["S"][:, 0:MAX_FRAMES], scalar1=z_sum[:], scalar2=None, op0=ALU.add
-        )
-        nc.vector.scalar_tensor_tensor(
-            out=dist[:, 0:MAX_FRAMES], in0=max_sum[:], scalar=2.0, in1=linear[:], op0=ALU.mult, op1=ALU.subtract
-        )
-        quantize_c(8)
-        for s in range(PSUM_BANKS):
-            enc_frame(s)
-
         least = keep.tile([P, 1], F32)
         logit = keep.tile([P, FRAMES], F32)
         expd = keep.tile([P, FRAMES], F32)
         total = keep.tile([P, 1], F32)
         inv_total = keep.tile([P, 1], F32)
         attn = keep.tile([P, FRAMES], F32)
+        quantize_w(0)
+        quantize_w(1)
+        quantize_c(0)
+        nc.vector.tensor_scalar(
+            out=linear[:], in0=bank["S"][:, 0:MAX_FRAMES], scalar1=z_sum[:], scalar2=None, op0=ALU.add
+        )
+        quantize_c(4)
+        nc.vector.scalar_tensor_tensor(
+            out=dist[:, 0:MAX_FRAMES], in0=max_sum[:], scalar=2.0, in1=linear[:], op0=ALU.mult, op1=ALU.subtract
+        )
+        nc.vector.reciprocal(out=inv_t1[:], in_=t1_bf[:])
+        quantize_c(8)
         nc.vector.tensor_reduce(out=least[:], in_=dist[:], axis=AX.X, op=ALU.min)
         nc.vector.tensor_scalar(
             out=logit[:], in0=dist[:], scalar1=least[:], scalar2=inv_t1[:], op0=ALU.subtract, op1=ALU.mult
         )
         nc.scalar.activation(out=expd[:], in_=logit[:], func=ACT.Exp, scale=-1.0, accum_out=total[:])
-        quantize_c(12)
-        quantize_c(16)
+        empty_bank(len(ORDER) - 2)
+        empty_bank(len(ORDER) - 1)
+        for s in range(PSUM_BANKS):
+            enc_frame(s)
         nc.vector.reciprocal(out=inv_total[:], in_=total[:])
         nc.vector.tensor_scalar(out=attn[:], in0=expd[:], scalar1=inv_total[:], scalar2=None, op0=ALU.mult)
 
         sums = (keep.tile([P, CH], F32, name="sum_even"), keep.tile([P, CH], F32, name="sum_odd"))
         sum_gpsimd = keep.tile([P, CH], F32)
+        both = keep.tile([P, CH], F32)
         weighted = keep.tile([P, len(SCALAR_FRAMES), CH], F32)
         result = keep.tile([P, CH], F32)
-        for s in range(FRAMES):
-            enc = bank["X", s]
-            weight = attn[:, s:s + 1]
+        HALF = CH // 2
+
+        def vector_frame(s, acc, start, cols):
+            nc.vector.scalar_tensor_tensor(
+                out=acc[:, cols], in0=bank["X", s][:, cols], scalar=attn[:, s:s + 1], in1=start[:, cols],
+                op0=ALU.mult, op1=ALU.add,
+            )
+
+        for s in range(FRAMES - 1):
             if s in SCALAR_FRAMES:
                 k = SCALAR_FRAMES.index(s)
-                nc.scalar.activation(out=weighted[:, k, :], in_=enc[:], func=ACT.Copy, scale=weight)
-                if k > 0:
+                nc.scalar.activation(out=weighted[:, k, :], in_=bank["X", s][:], func=ACT.Copy, scale=attn[:, s:s + 1])
+                if k > 1:
                     nc.gpsimd.tensor_tensor(
                         out=sum_gpsimd[:],
-                        in0=(weighted[:, 0, :] if k == 1 else sum_gpsimd[:]),
+                        in0=(weighted[:, 1, :] if k == 2 else sum_gpsimd[:]),
                         in1=weighted[:, k, :],
                         op=ALU.add,
                     )
             else:
                 k = VECTOR_FRAMES.index(s)
-                acc = sums[k % 2]
+                start = bias_bc if k == 0 else weighted[:, 0, :] if k == 1 else sums[k % 2]
+                vector_frame(s, sums[k % 2], start, slice(0, CH))
                 if k == 1:
-                    nc.vector.tensor_scalar(out=acc[:], in0=enc[:], scalar1=weight, scalar2=None, op0=ALU.mult)
-                else:
-                    nc.vector.scalar_tensor_tensor(
-                        out=acc[:],
-                        in0=enc[:],
-                        scalar=weight,
-                        in1=(bias_bc[:] if k == 0 else acc[:]),
-                        op0=ALU.mult,
-                        op1=ALU.add,
-                    )
+                    quantize_c(12)
+                elif k == 2:
+                    quantize_c(16)
             if s + PSUM_BANKS < FRAMES:
                 enc_frame(s + PSUM_BANKS)
-        nc.vector.tensor_tensor(out=sums[0][:], in0=sums[0][:], in1=sums[1][:], op=ALU.add)
-        nc.vector.tensor_tensor(out=result[:], in0=sums[0][:], in1=sum_gpsimd[:], op=ALU.add)
-        nc.sync.dma_start(out=out[:, :], in_=result[:])
+        nc.vector.tensor_tensor(out=both[:], in0=sums[0][:], in1=sum_gpsimd[:], op=ALU.add)
+        halves = (slice(0, HALF), slice(HALF, CH))
+        for cols in halves:
+            vector_frame(FRAMES - 1, sums[1], sums[1], cols)
+        for cols in halves:
+            nc.vector.tensor_tensor(out=result[:, cols], in0=sums[1][:, cols], in1=both[:, cols], op=ALU.add)
+            nc.sync.dma_start(out=out[:, cols], in_=result[:, cols])

@@ -29,10 +29,12 @@ ORDER = (
     ("W", 0), ("W", 1), ("W", 2), ("W", 3), ("C", 0), ("C", 1), ("C", 2), ("C", 3), ("C", 4), ("C", 5),
     ("C", 6), ("C", 7), ("C", 8),
 )
-WARM_UPS = 3
+SCALAR_TAPS = 1
+WARM_UPS = 5
 ROTATING = 6
 SUM_BANK = 6
 Z_BANK = 7
+ENC_BANKS = (3, 4, 5, 7, 6, 0, 1, 2)
 
 
 def tile_dynamix_pa_kernel(tc, context, D, z, conv_w, conv_b, t1, out):
@@ -68,9 +70,11 @@ def tile_dynamix_pa_kernel(tc, context, D, z, conv_w, conv_b, t1, out):
         load_d(3)
         for c in range(4):
             nc.sync.dma_start(out=w_sb[:, c, :], in_=conv_w[c * P:(c + 1) * P].rearrange("o i t -> o (i t)"))
-        for g in LOAD_ORDER:
+        for g in LOAD_ORDER[0:4]:
             load_frames(g)
         nc.sync.dma_start(out=t1_bf[:], in_=t1.partition_broadcast(P))
+        for g in LOAD_ORDER[4:]:
+            load_frames(g)
         nc.sync.dma_start(out=bias_bc[:], in_=conv_b.partition_broadcast(P))
 
         bank = {}
@@ -115,10 +119,12 @@ def tile_dynamix_pa_kernel(tc, context, D, z, conv_w, conv_b, t1, out):
 
         def part_taps(c):
             for t in range(2):
-                nc.vector.tensor_copy(
-                    out=w_taps[:, c, t, :, :].rearrange("o u (q e) -> o u q e", e=2),
-                    in_=w_sb[:, c, :].rearrange("o (q u e t) -> o t u q e", u=2, e=2, t=2)[:, t],
-                )
+                dst = w_taps[:, c, t, :, :].rearrange("o u (q e) -> o u q e", e=2)
+                src = w_sb[:, c, :].rearrange("o (q u e t) -> o t u q e", u=2, e=2, t=2)[:, t]
+                if c == SCALAR_TAPS:
+                    nc.scalar.copy(out=dst, in_=src)
+                else:
+                    nc.vector.tensor_copy(out=dst, in_=src)
 
         new_bank("Z", "z_obs", Z_BANK)
         zeros = keep.tile([P, P], F32)
@@ -134,6 +140,7 @@ def tile_dynamix_pa_kernel(tc, context, D, z, conv_w, conv_b, t1, out):
         copy_d(0)
         transpose_d(1)
         copy_d(1)
+        warm_up()
         warm_up()
         transpose_d(2)
         copy_d(2)
@@ -191,6 +198,7 @@ def tile_dynamix_pa_kernel(tc, context, D, z, conv_w, conv_b, t1, out):
         dist = keep.tile([P, FRAMES], F32)
         unused = keep.tile([P, FRAMES, CH], BF16)
         inv_t1 = keep.tile([P, 1], F32)
+        two_inv_t1 = keep.tile([P, 1], F32)
 
         def max_frame(s):
             nc.vector.scalar_tensor_tensor(
@@ -200,7 +208,7 @@ def tile_dynamix_pa_kernel(tc, context, D, z, conv_w, conv_b, t1, out):
 
         def abs_frame(s):
             nc.scalar.activation(out=unused[:, s, :], in_=diff[:, s - MAX_FRAMES, :], func=ACT.Abs,
-                                 accum_out=dist[:, s:s + 1])
+                                 scale=inv_t1[:], accum_out=dist[:, s:s + 1])
 
         def sum_frame(s):
             for k in range(4):
@@ -221,32 +229,6 @@ def tile_dynamix_pa_kernel(tc, context, D, z, conv_w, conv_b, t1, out):
                 in_=c_grouped[:, s0 * CH:s1 * CH],
             )
 
-        new_bank("S", "c_sums", SUM_BANK)
-        nc.vector.tensor_copy(out=z_obs_sb[:], in_=bank["Z"][:])
-        for s in range(MAX_FRAMES, FRAMES):
-            nc.gpsimd.tensor_tensor(
-                out=diff[:, s - MAX_FRAMES, :], in0=c_sb[:, s, :], in1=z_obs_sb[:], op=ALU.subtract
-            )
-        for n in range(ROTATING - 2):
-            transpose_bank(n)
-        for n in range(len(ORDER) - 3):
-            empty_bank(n)
-            kind, j = ORDER[n]
-            if kind == "C" and 2 * j < MAX_FRAMES:
-                sum_frame(2 * j)
-                sum_frame(2 * j + 1)
-            if n + ROTATING - 2 < len(ORDER):
-                transpose_bank(n + ROTATING - 2)
-            if n == 8:
-                nc.scalar.activation(out=unused[:, 0, :], in_=z_obs_sb[:], func=ACT.Copy, accum_out=z_sum[:])
-            if 4 <= n < 4 + FRAMES - MAX_FRAMES:
-                abs_frame(MAX_FRAMES + n - 4)
-            if n < MAX_FRAMES:
-                max_frame(n)
-        empty_bank(len(ORDER) - 3)
-
-        ENC_BANKS = (3, 4, 6, 7, 5, 0, 1, 2)
-
         def enc_frame(s):
             target = new_bank(("X", s), "enc%d" % s, ENC_BANKS[s % PSUM_BANKS])
             for t in range(2):
@@ -260,32 +242,58 @@ def tile_dynamix_pa_kernel(tc, context, D, z, conv_w, conv_b, t1, out):
                     stop=(t == 1),
                 )
 
+        new_bank("S", "c_sums", SUM_BANK)
+        nc.vector.tensor_scalar(
+            out=z_obs_sb[:], in0=bank["Z"][:], scalar1=1.0, scalar2=None, op0=ALU.mult, op1=ALU.add, accum_out=z_sum[:]
+        )
+        for s in range(MAX_FRAMES, FRAMES):
+            nc.gpsimd.tensor_tensor(
+                out=diff[:, s - MAX_FRAMES, :], in0=c_sb[:, s, :], in1=z_obs_sb[:], op=ALU.subtract
+            )
+        for n in range(ROTATING - 2):
+            transpose_bank(n)
+        for n in range(10):
+            empty_bank(n)
+            kind, j = ORDER[n]
+            if kind == "C" and 2 * j < MAX_FRAMES:
+                sum_frame(2 * j)
+                sum_frame(2 * j + 1)
+            if n + ROTATING - 2 < len(ORDER):
+                transpose_bank(n + ROTATING - 2)
+            max_frame(n)
+            if n == 3:
+                nc.vector.reciprocal(out=inv_t1[:], in_=t1_bf[:])
+                nc.vector.tensor_scalar(out=two_inv_t1[:], in0=inv_t1[:], scalar1=2.0, scalar2=None, op0=ALU.mult)
+            elif n == 6:
+                quantize_w(0)
+                quantize_w(1)
+                quantize_c(0)
+            if n >= 7:
+                enc_frame(n - 7)
+            if n >= 5:
+                abs_frame(n + 5)
+        abs_frame(15)
+
         least = keep.tile([P, 1], F32)
-        logit = keep.tile([P, FRAMES], F32)
         expd = keep.tile([P, FRAMES], F32)
         total = keep.tile([P, 1], F32)
         inv_total = keep.tile([P, 1], F32)
         attn = keep.tile([P, FRAMES], F32)
-        quantize_w(0)
-        quantize_w(1)
-        quantize_c(0)
         nc.vector.tensor_scalar(
-            out=linear[:], in0=bank["S"][:, 0:MAX_FRAMES], scalar1=z_sum[:], scalar2=None, op0=ALU.add
+            out=linear[:], in0=bank["S"][:, 0:MAX_FRAMES], scalar1=z_sum[:], scalar2=inv_t1[:], op0=ALU.add, op1=ALU.mult
         )
         quantize_c(4)
         nc.vector.scalar_tensor_tensor(
-            out=dist[:, 0:MAX_FRAMES], in0=max_sum[:], scalar=2.0, in1=linear[:], op0=ALU.mult, op1=ALU.subtract
+            out=dist[:, 0:MAX_FRAMES], in0=max_sum[:], scalar=two_inv_t1[:], in1=linear[:], op0=ALU.mult,
+            op1=ALU.subtract,
         )
-        nc.vector.reciprocal(out=inv_t1[:], in_=t1_bf[:])
-        quantize_c(8)
         nc.vector.tensor_reduce(out=least[:], in_=dist[:], axis=AX.X, op=ALU.min)
-        nc.vector.tensor_scalar(
-            out=logit[:], in0=dist[:], scalar1=least[:], scalar2=inv_t1[:], op0=ALU.subtract, op1=ALU.mult
-        )
-        nc.scalar.activation(out=expd[:], in_=logit[:], func=ACT.Exp, scale=-1.0, accum_out=total[:])
-        empty_bank(len(ORDER) - 2)
-        empty_bank(len(ORDER) - 1)
-        for s in range(PSUM_BANKS):
+        empty_bank(10)
+        nc.scalar.activation(out=expd[:], in_=dist[:], func=ACT.Exp, scale=-1.0, bias=least[:], accum_out=total[:])
+        quantize_c(8)
+        empty_bank(11)
+        empty_bank(12)
+        for s in range(3, PSUM_BANKS):
             enc_frame(s)
         nc.vector.reciprocal(out=inv_total[:], in_=total[:])
         nc.vector.tensor_scalar(out=attn[:], in0=expd[:], scalar1=inv_total[:], scalar2=None, op0=ALU.mult)
@@ -324,10 +332,10 @@ def tile_dynamix_pa_kernel(tc, context, D, z, conv_w, conv_b, t1, out):
                     quantize_c(16)
             if s + PSUM_BANKS < FRAMES:
                 enc_frame(s + PSUM_BANKS)
-        nc.vector.tensor_tensor(out=both[:], in0=sums[0][:], in1=sum_gpsimd[:], op=ALU.add)
         halves = (slice(0, HALF), slice(HALF, CH))
         for cols in halves:
             vector_frame(FRAMES - 1, sums[1], sums[1], cols)
+        nc.vector.tensor_tensor(out=both[:], in0=sums[0][:], in1=sum_gpsimd[:], op=ALU.add)
         for cols in halves:
             nc.vector.tensor_tensor(out=result[:, cols], in0=sums[1][:, cols], in1=both[:, cols], op=ALU.add)
             nc.sync.dma_start(out=out[:, cols], in_=result[:, cols])

@@ -21,16 +21,17 @@ PAIRS = LOADED // 2
 PSUM_BANKS = 8
 FLOPS = 2 * FRAMES * P * CH * CH * 2 + 2 * CH * LATENT * P
 
-MAX_FRAMES = 10
-LOAD_ORDER = (5, 0, 1, 6, 2, 3, 7, 4, 8)
-SCALAR_FRAMES = (1, 3, 5, 7, 9)
+MAX_FRAMES = 12
+LOAD_ORDER = (0, 6, 1, 2, 7, 3, 4, 5, 8)
+SUM_COLUMNS = 32
+SCALAR_FRAMES = (1, 2, 3, 7, 9, 11)
 VECTOR_FRAMES = tuple(s for s in range(FRAMES) if s not in SCALAR_FRAMES)
 ORDER = (
     ("W", 0), ("W", 1), ("W", 2), ("W", 3), ("C", 0), ("C", 1), ("C", 2), ("C", 3), ("C", 4), ("C", 5),
     ("C", 6), ("C", 7), ("C", 8),
 )
-SCALAR_TAPS = 1
-WARM_UPS = 5
+TAP_ENGINES = ("gpsimd", "vector", "scalar", "gpsimd")
+WARM_UPS = 3
 ROTATING = 6
 SUM_BANK = 6
 Z_BANK = 7
@@ -46,7 +47,7 @@ def tile_dynamix_pa_kernel(tc, context, D, z, conv_w, conv_b, t1, out):
 
         ident = keep.tile([P, P], F32)
         make_identity(nc, ident[:])
-        ones = keep.tile([P, 1], BF16)
+        ones = keep.tile([P, SUM_COLUMNS], BF16)
         nc.vector.memset(ones[:], 1.0)
 
         d_sb = keep.tile([P, 4, LATENT], BF16)
@@ -70,11 +71,9 @@ def tile_dynamix_pa_kernel(tc, context, D, z, conv_w, conv_b, t1, out):
         load_d(3)
         for c in range(4):
             nc.sync.dma_start(out=w_sb[:, c, :], in_=conv_w[c * P:(c + 1) * P].rearrange("o i t -> o (i t)"))
-        for g in LOAD_ORDER[0:4]:
+        for g in LOAD_ORDER:
             load_frames(g)
         nc.sync.dma_start(out=t1_bf[:], in_=t1.partition_broadcast(P))
-        for g in LOAD_ORDER[4:]:
-            load_frames(g)
         nc.sync.dma_start(out=bias_bc[:], in_=conv_b.partition_broadcast(P))
 
         bank = {}
@@ -121,10 +120,12 @@ def tile_dynamix_pa_kernel(tc, context, D, z, conv_w, conv_b, t1, out):
             for t in range(2):
                 dst = w_taps[:, c, t, :, :].rearrange("o u (q e) -> o u q e", e=2)
                 src = w_sb[:, c, :].rearrange("o (q u e t) -> o t u q e", u=2, e=2, t=2)[:, t]
-                if c == SCALAR_TAPS:
+                if TAP_ENGINES[c] == "scalar":
                     nc.scalar.copy(out=dst, in_=src)
-                else:
+                elif TAP_ENGINES[c] == "vector":
                     nc.vector.tensor_copy(out=dst, in_=src)
+                else:
+                    nc.gpsimd.tensor_scalar(out=dst, in0=src, scalar1=1.0, scalar2=0.0, op0=ALU.mult, op1=ALU.add)
 
         new_bank("Z", "z_obs", Z_BANK)
         zeros = keep.tile([P, P], F32)
@@ -140,7 +141,6 @@ def tile_dynamix_pa_kernel(tc, context, D, z, conv_w, conv_b, t1, out):
         copy_d(0)
         transpose_d(1)
         copy_d(1)
-        warm_up()
         warm_up()
         transpose_d(2)
         copy_d(2)
@@ -213,7 +213,8 @@ def tile_dynamix_pa_kernel(tc, context, D, z, conv_w, conv_b, t1, out):
         def sum_frame(s):
             for k in range(4):
                 nc.tensor.matmul(
-                    bank["S"][:, s:s + 1], lhsT=c_by_place[:, s, :, k], rhs=ones[:], start=(k == 0), stop=(k == 3)
+                    bank["S"][:, s * SUM_COLUMNS:(s + 1) * SUM_COLUMNS], lhsT=c_by_place[:, s, :, k], rhs=ones[:],
+                    start=(k == 0), stop=(k == 3),
                 )
 
         def quantize_w(t):
@@ -254,25 +255,26 @@ def tile_dynamix_pa_kernel(tc, context, D, z, conv_w, conv_b, t1, out):
             transpose_bank(n)
         for n in range(10):
             empty_bank(n)
-            kind, j = ORDER[n]
-            if kind == "C" and 2 * j < MAX_FRAMES:
-                sum_frame(2 * j)
-                sum_frame(2 * j + 1)
             if n + ROTATING - 2 < len(ORDER):
                 transpose_bank(n + ROTATING - 2)
             max_frame(n)
-            if n == 3:
+            if n == 6:
+                for s in range(4):
+                    sum_frame(s)
+            elif n == 7:
                 nc.vector.reciprocal(out=inv_t1[:], in_=t1_bf[:])
                 nc.vector.tensor_scalar(out=two_inv_t1[:], in0=inv_t1[:], scalar1=2.0, scalar2=None, op0=ALU.mult)
-            elif n == 6:
                 quantize_w(0)
                 quantize_w(1)
                 quantize_c(0)
-            if n >= 7:
-                enc_frame(n - 7)
-            if n >= 5:
-                abs_frame(n + 5)
-        abs_frame(15)
+        for s in range(10, MAX_FRAMES):
+            max_frame(s)
+        for s in range(4, MAX_FRAMES):
+            sum_frame(s)
+        for s in range(MAX_FRAMES, FRAMES):
+            abs_frame(s)
+        for n in range(10, len(ORDER)):
+            empty_bank(n)
 
         least = keep.tile([P, 1], F32)
         expd = keep.tile([P, FRAMES], F32)
@@ -280,7 +282,7 @@ def tile_dynamix_pa_kernel(tc, context, D, z, conv_w, conv_b, t1, out):
         inv_total = keep.tile([P, 1], F32)
         attn = keep.tile([P, FRAMES], F32)
         nc.vector.tensor_scalar(
-            out=linear[:], in0=bank["S"][:, 0:MAX_FRAMES], scalar1=z_sum[:], scalar2=inv_t1[:], op0=ALU.add, op1=ALU.mult
+            out=linear[:], in0=bank["S"][:, 0:MAX_FRAMES * SUM_COLUMNS:SUM_COLUMNS], scalar1=z_sum[:], scalar2=inv_t1[:], op0=ALU.add, op1=ALU.mult
         )
         quantize_c(4)
         nc.vector.scalar_tensor_tensor(
@@ -288,12 +290,9 @@ def tile_dynamix_pa_kernel(tc, context, D, z, conv_w, conv_b, t1, out):
             op1=ALU.subtract,
         )
         nc.vector.tensor_reduce(out=least[:], in_=dist[:], axis=AX.X, op=ALU.min)
-        empty_bank(10)
         nc.scalar.activation(out=expd[:], in_=dist[:], func=ACT.Exp, scale=-1.0, bias=least[:], accum_out=total[:])
         quantize_c(8)
-        empty_bank(11)
-        empty_bank(12)
-        for s in range(3, PSUM_BANKS):
+        for s in range(PSUM_BANKS):
             enc_frame(s)
         nc.vector.reciprocal(out=inv_total[:], in_=total[:])
         nc.vector.tensor_scalar(out=attn[:], in0=expd[:], scalar1=inv_total[:], scalar2=None, op0=ALU.mult)
@@ -304,6 +303,8 @@ def tile_dynamix_pa_kernel(tc, context, D, z, conv_w, conv_b, t1, out):
         weighted = keep.tile([P, len(SCALAR_FRAMES), CH], F32)
         result = keep.tile([P, CH], F32)
         HALF = CH // 2
+        GPSIMD_ADDS = (1, 3, 4, 5)
+        SECOND_SUM = (2, 4, 6, 8)
 
         def vector_frame(s, acc, start, cols):
             nc.vector.scalar_tensor_tensor(
@@ -315,18 +316,19 @@ def tile_dynamix_pa_kernel(tc, context, D, z, conv_w, conv_b, t1, out):
             if s in SCALAR_FRAMES:
                 k = SCALAR_FRAMES.index(s)
                 nc.scalar.activation(out=weighted[:, k, :], in_=bank["X", s][:], func=ACT.Copy, scale=attn[:, s:s + 1])
-                if k > 1:
+                if k in GPSIMD_ADDS:
                     nc.gpsimd.tensor_tensor(
                         out=sum_gpsimd[:],
-                        in0=(weighted[:, 1, :] if k == 2 else sum_gpsimd[:]),
+                        in0=(weighted[:, 0, :] if k == 1 else sum_gpsimd[:]),
                         in1=weighted[:, k, :],
                         op=ALU.add,
                     )
             else:
                 k = VECTOR_FRAMES.index(s)
-                start = bias_bc if k == 0 else weighted[:, 0, :] if k == 1 else sums[k % 2]
-                vector_frame(s, sums[k % 2], start, slice(0, CH))
-                if k == 1:
+                acc = sums[1] if k in SECOND_SUM else sums[0]
+                start = bias_bc if k == 0 else weighted[:, 2, :] if k == 2 else acc
+                vector_frame(s, acc, start, slice(0, CH))
+                if k == 0:
                     quantize_c(12)
                 elif k == 2:
                     quantize_c(16)
@@ -334,8 +336,8 @@ def tile_dynamix_pa_kernel(tc, context, D, z, conv_w, conv_b, t1, out):
                 enc_frame(s + PSUM_BANKS)
         halves = (slice(0, HALF), slice(HALF, CH))
         for cols in halves:
-            vector_frame(FRAMES - 1, sums[1], sums[1], cols)
-        nc.vector.tensor_tensor(out=both[:], in0=sums[0][:], in1=sum_gpsimd[:], op=ALU.add)
+            vector_frame(FRAMES - 1, sums[0], sums[0], cols)
+        nc.vector.tensor_tensor(out=both[:], in0=sums[1][:], in1=sum_gpsimd[:], op=ALU.add)
         for cols in halves:
-            nc.vector.tensor_tensor(out=result[:, cols], in0=sums[1][:, cols], in1=both[:, cols], op=ALU.add)
+            nc.vector.tensor_tensor(out=result[:, cols], in0=sums[0][:, cols], in1=both[:, cols], op=ALU.add)
             nc.sync.dma_start(out=out[:, cols], in_=result[:, cols])

@@ -21,16 +21,17 @@ PAIRS = LOADED // 2
 PSUM_BANKS = 8
 FLOPS = 2 * FRAMES * P * CH * CH * 2 + 2 * CH * LATENT * P
 
-MAX_FRAMES = 12
+MAX_FRAMES = 11
+ABS_FRAMES = (12, 13, 14, 15, 11)
 LOAD_ORDER = (0, 6, 1, 2, 7, 3, 4, 5, 8)
 SUM_COLUMNS = 32
-SCALAR_FRAMES = (1, 2, 3, 7, 9, 11)
+SCALAR_FRAMES = (1, 2, 3, 5, 7, 9)
 VECTOR_FRAMES = tuple(s for s in range(FRAMES) if s not in SCALAR_FRAMES)
 ORDER = (
     ("W", 0), ("W", 1), ("W", 2), ("W", 3), ("C", 0), ("C", 1), ("C", 2), ("C", 3), ("C", 4), ("C", 5),
     ("C", 6), ("C", 7), ("C", 8),
 )
-TAP_ENGINES = ("gpsimd", "vector", "scalar", "gpsimd")
+TAP_ENGINES = ("gpsimd", "vector", "scalar", "vector")
 WARM_UPS = 3
 ROTATING = 6
 SUM_BANK = 6
@@ -247,7 +248,7 @@ def tile_dynamix_pa_kernel(tc, context, D, z, conv_w, conv_b, t1, out):
         nc.vector.tensor_scalar(
             out=z_obs_sb[:], in0=bank["Z"][:], scalar1=1.0, scalar2=None, op0=ALU.mult, op1=ALU.add, accum_out=z_sum[:]
         )
-        for s in range(MAX_FRAMES, FRAMES):
+        for s in ABS_FRAMES:
             nc.gpsimd.tensor_tensor(
                 out=diff[:, s - MAX_FRAMES, :], in0=c_sb[:, s, :], in1=z_obs_sb[:], op=ALU.subtract
             )
@@ -261,20 +262,19 @@ def tile_dynamix_pa_kernel(tc, context, D, z, conv_w, conv_b, t1, out):
             if n == 6:
                 for s in range(4):
                     sum_frame(s)
-            elif n == 7:
+            elif n == 8:
                 nc.vector.reciprocal(out=inv_t1[:], in_=t1_bf[:])
                 nc.vector.tensor_scalar(out=two_inv_t1[:], in0=inv_t1[:], scalar1=2.0, scalar2=None, op0=ALU.mult)
                 quantize_w(0)
                 quantize_w(1)
                 quantize_c(0)
-        for s in range(10, MAX_FRAMES):
-            max_frame(s)
+        max_frame(10)
         for s in range(4, MAX_FRAMES):
             sum_frame(s)
-        for s in range(MAX_FRAMES, FRAMES):
+        for s in ABS_FRAMES:
             abs_frame(s)
-        for n in range(10, len(ORDER)):
-            empty_bank(n)
+        empty_bank(10)
+        empty_bank(11)
 
         least = keep.tile([P, 1], F32)
         expd = keep.tile([P, FRAMES], F32)
@@ -291,53 +291,64 @@ def tile_dynamix_pa_kernel(tc, context, D, z, conv_w, conv_b, t1, out):
         )
         nc.vector.tensor_reduce(out=least[:], in_=dist[:], axis=AX.X, op=ALU.min)
         nc.scalar.activation(out=expd[:], in_=dist[:], func=ACT.Exp, scale=-1.0, bias=least[:], accum_out=total[:])
+        empty_bank(12)
         quantize_c(8)
         for s in range(PSUM_BANKS):
             enc_frame(s)
         nc.vector.reciprocal(out=inv_total[:], in_=total[:])
         nc.vector.tensor_scalar(out=attn[:], in0=expd[:], scalar1=inv_total[:], scalar2=None, op0=ALU.mult)
+        quantize_c(12)
 
-        sums = (keep.tile([P, CH], F32, name="sum_even"), keep.tile([P, CH], F32, name="sum_odd"))
+        sums = (keep.tile([P, CH], F32, name="sum_a"), keep.tile([P, CH], F32, name="sum_b"))
         sum_gpsimd = keep.tile([P, CH], F32)
-        both = keep.tile([P, CH], F32)
         weighted = keep.tile([P, len(SCALAR_FRAMES), CH], F32)
+        partial = keep.tile([P, CH], F32)
         result = keep.tile([P, CH], F32)
-        HALF = CH // 2
-        GPSIMD_ADDS = (1, 3, 4, 5)
-        SECOND_SUM = (2, 4, 6, 8)
 
-        def vector_frame(s, acc, start, cols):
+        STARTS = (0, 2)
+
+        def vector_frame(k, cols):
+            s = VECTOR_FRAMES[k]
+            acc = sums[k % 2]
+            start = weighted[:, STARTS[k], :] if k < 2 else acc
             nc.vector.scalar_tensor_tensor(
-                out=acc[:, cols], in0=bank["X", s][:, cols], scalar=attn[:, s:s + 1], in1=start[:, cols],
+                out=acc[:, cols], in0=bank["X", s][:, cols], scalar=expd[:, s:s + 1], in1=start[:, cols],
                 op0=ALU.mult, op1=ALU.add,
             )
 
-        for s in range(FRAMES - 1):
+        def scalar_frame(k):
+            s = SCALAR_FRAMES[k]
+            weight = expd if k in STARTS else attn
+            nc.scalar.activation(out=weighted[:, k, :], in_=bank["X", s][:], func=ACT.Copy, scale=weight[:, s:s + 1])
+            if k not in STARTS:
+                nc.gpsimd.tensor_tensor(
+                    out=sum_gpsimd[:], in0=(bias_bc[:] if k == 1 else sum_gpsimd[:]), in1=weighted[:, k, :], op=ALU.add
+                )
+
+        def over_total(dst, src, add, cols):
+            nc.vector.scalar_tensor_tensor(
+                out=dst[:, cols], in0=src[:, cols], scalar=inv_total[:], in1=add[:, cols], op0=ALU.mult, op1=ALU.add
+            )
+
+        whole = slice(0, CH)
+        halves = (slice(0, CH // 2), slice(CH // 2, CH))
+        started = PSUM_BANKS
+        done = set()
+        for s in (1, 0) + tuple(range(2, FRAMES - 1)):
             if s in SCALAR_FRAMES:
-                k = SCALAR_FRAMES.index(s)
-                nc.scalar.activation(out=weighted[:, k, :], in_=bank["X", s][:], func=ACT.Copy, scale=attn[:, s:s + 1])
-                if k in GPSIMD_ADDS:
-                    nc.gpsimd.tensor_tensor(
-                        out=sum_gpsimd[:],
-                        in0=(weighted[:, 0, :] if k == 1 else sum_gpsimd[:]),
-                        in1=weighted[:, k, :],
-                        op=ALU.add,
-                    )
+                scalar_frame(SCALAR_FRAMES.index(s))
             else:
-                k = VECTOR_FRAMES.index(s)
-                acc = sums[1] if k in SECOND_SUM else sums[0]
-                start = bias_bc if k == 0 else weighted[:, 2, :] if k == 2 else acc
-                vector_frame(s, acc, start, slice(0, CH))
-                if k == 0:
-                    quantize_c(12)
-                elif k == 2:
-                    quantize_c(16)
-            if s + PSUM_BANKS < FRAMES:
-                enc_frame(s + PSUM_BANKS)
-        halves = (slice(0, HALF), slice(HALF, CH))
+                vector_frame(VECTOR_FRAMES.index(s), whole)
+            if s == 0:
+                quantize_c(16)
+            done.add(s)
+            while started < FRAMES and started - PSUM_BANKS in done:
+                enc_frame(started)
+                started += 1
         for cols in halves:
-            vector_frame(FRAMES - 1, sums[0], sums[0], cols)
-        nc.vector.tensor_tensor(out=both[:], in0=sums[1][:], in1=sum_gpsimd[:], op=ALU.add)
+            vector_frame(len(VECTOR_FRAMES) - 1, cols)
         for cols in halves:
-            nc.vector.tensor_tensor(out=result[:, cols], in0=sums[0][:, cols], in1=both[:, cols], op=ALU.add)
+            over_total(partial, sums[0], sum_gpsimd, cols)
+        for cols in halves:
+            over_total(result, sums[1], partial, cols)
             nc.sync.dma_start(out=out[:, cols], in_=result[:, cols])

@@ -31,7 +31,7 @@ ORDER = (
     ("W", 0), ("W", 1), ("W", 2), ("W", 3), ("C", 0), ("C", 1), ("C", 2), ("C", 3), ("C", 4), ("C", 5),
     ("C", 6), ("C", 7), ("C", 8),
 )
-TAP_ENGINES = ("gpsimd", "vector", "scalar", "vector")
+TAP_ENGINES = ("vector", "vector", "scalar", "vector")
 WARM_UPS = 3
 ROTATING = 6
 SUM_BANK = 6
@@ -123,10 +123,8 @@ def tile_dynamix_pa_kernel(tc, context, D, z, conv_w, conv_b, t1, out):
                 src = w_sb[:, c, :].rearrange("o (q u e t) -> o t u q e", u=2, e=2, t=2)[:, t]
                 if TAP_ENGINES[c] == "scalar":
                     nc.scalar.copy(out=dst, in_=src)
-                elif TAP_ENGINES[c] == "vector":
-                    nc.vector.tensor_copy(out=dst, in_=src)
                 else:
-                    nc.gpsimd.tensor_scalar(out=dst, in0=src, scalar1=1.0, scalar2=0.0, op0=ALU.mult, op1=ALU.add)
+                    nc.vector.tensor_copy(out=dst, in_=src)
 
         new_bank("Z", "z_obs", Z_BANK)
         zeros = keep.tile([P, P], F32)
@@ -264,10 +262,10 @@ def tile_dynamix_pa_kernel(tc, context, D, z, conv_w, conv_b, t1, out):
                     sum_frame(s)
             elif n == 8:
                 nc.vector.reciprocal(out=inv_t1[:], in_=t1_bf[:])
-                nc.vector.tensor_scalar(out=two_inv_t1[:], in0=inv_t1[:], scalar1=2.0, scalar2=None, op0=ALU.mult)
-                quantize_w(0)
-                quantize_w(1)
-                quantize_c(0)
+        nc.scalar.activation(out=two_inv_t1[:], in_=inv_t1[:], func=ACT.Copy, scale=2.0)
+        quantize_w(0)
+        quantize_w(1)
+        quantize_c(0)
         max_frame(10)
         for s in range(4, MAX_FRAMES):
             sum_frame(s)
@@ -298,6 +296,7 @@ def tile_dynamix_pa_kernel(tc, context, D, z, conv_w, conv_b, t1, out):
         nc.vector.reciprocal(out=inv_total[:], in_=total[:])
         nc.vector.tensor_scalar(out=attn[:], in0=expd[:], scalar1=inv_total[:], scalar2=None, op0=ALU.mult)
         quantize_c(12)
+        quantize_c(16)
 
         sums = (keep.tile([P, CH], F32, name="sum_a"), keep.tile([P, CH], F32, name="sum_b"))
         sum_gpsimd = keep.tile([P, CH], F32)
@@ -339,8 +338,6 @@ def tile_dynamix_pa_kernel(tc, context, D, z, conv_w, conv_b, t1, out):
                 scalar_frame(SCALAR_FRAMES.index(s))
             else:
                 vector_frame(VECTOR_FRAMES.index(s), whole)
-            if s == 0:
-                quantize_c(16)
             done.add(s)
             while started < FRAMES and started - PSUM_BANKS in done:
                 enc_frame(started)

@@ -24,12 +24,12 @@ FLOPS = 2 * FRAMES * P * CH * CH * 2 + 2 * CH * LATENT * P
 MAX_FRAMES = 11
 ABS_FRAMES = (12, 13, 14, 15, 11)
 LOAD_ORDER = (0, 6, 1, 2, 7, 3, 4, 5, 8)
-SUM_COLUMNS = 32
+SUM_COLUMNS = 512 // MAX_FRAMES // 2 * 2
 SCALAR_FRAMES = (1, 2, 3, 5, 7, 9)
 VECTOR_FRAMES = tuple(s for s in range(FRAMES) if s not in SCALAR_FRAMES)
 ORDER = (
-    ("W", 0), ("W", 1), ("W", 2), ("W", 3), ("C", 0), ("C", 1), ("C", 2), ("C", 3), ("C", 4), ("C", 5),
-    ("C", 6), ("C", 7), ("C", 8),
+    ("W", 0), ("W", 1), ("W", 2), ("W", 3), ("C", 0), ("C", 6), ("C", 1), ("C", 2), ("C", 7), ("C", 3),
+    ("C", 4), ("C", 5), ("C", 8),
 )
 TAP_ENGINES = ("vector", "vector", "scalar", "vector")
 WARM_UPS = 3
@@ -48,12 +48,15 @@ def tile_dynamix_pa_kernel(tc, context, D, z, conv_w, conv_b, t1, out):
 
         ident = keep.tile([P, P], F32)
         make_identity(nc, ident[:])
-        ones = keep.tile([P, SUM_COLUMNS], BF16)
+        zeros = keep.tile([P, P], F32)
+        nc.vector.memset(zeros[:], 0.0)
+        t1_row = keep.tile([P, 2], BF16)
+        nc.vector.memset(t1_row[:], 0.0)
+        ones = keep.tile([P, P], BF16)
         nc.vector.memset(ones[:], 1.0)
 
         d_sb = keep.tile([P, 4, LATENT], BF16)
         z_sb = keep.tile([P, 4, 2, P], BF16)
-        t1_bf = keep.tile([P, 1], BF16)
         c_sb = keep.tile([P, LOADED, CH], BF16)
         w_sb = keep.tile([P, 4, 2 * CH], BF16)
         bias_bc = keep.tile([P, CH], BF16)
@@ -65,6 +68,7 @@ def tile_dynamix_pa_kernel(tc, context, D, z, conv_w, conv_b, t1, out):
             s0, s1 = 2 * g, min(2 * g + 2, LOADED)
             nc.sync.dma_start(out=c_sb[:, s0:s1, :], in_=context[s0:s1].rearrange("s b i -> b s i"))
 
+        nc.scalar.dma_start(out=t1_row[0:1, 0:1], in_=t1.rearrange("(a b) -> a b", a=1))
         load_d(0)
         load_d(1)
         nc.sync.dma_start(out=z_sb[:], in_=z.rearrange("(u q e) b -> q u e b", u=4, e=2))
@@ -74,7 +78,6 @@ def tile_dynamix_pa_kernel(tc, context, D, z, conv_w, conv_b, t1, out):
             nc.sync.dma_start(out=w_sb[:, c, :], in_=conv_w[c * P:(c + 1) * P].rearrange("o i t -> o (i t)"))
         for g in LOAD_ORDER:
             load_frames(g)
-        nc.sync.dma_start(out=t1_bf[:], in_=t1.partition_broadcast(P))
         nc.sync.dma_start(out=bias_bc[:], in_=conv_b.partition_broadcast(P))
 
         bank = {}
@@ -127,8 +130,6 @@ def tile_dynamix_pa_kernel(tc, context, D, z, conv_w, conv_b, t1, out):
                     nc.vector.tensor_copy(out=dst, in_=src)
 
         new_bank("Z", "z_obs", Z_BANK)
-        zeros = keep.tile([P, P], F32)
-        nc.vector.memset(zeros[:], 0.0)
         new_bank("warm", "warm", ROTATING - 1)
 
         def warm_up():
@@ -148,6 +149,8 @@ def tile_dynamix_pa_kernel(tc, context, D, z, conv_w, conv_b, t1, out):
         copy_d(3)
         z_obs_half(0, 4, 8)
         z_obs_half(1, 0, 8)
+        new_bank("t1", "t1_bc", SUM_BANK)
+        nc.tensor.matmul(bank["t1"][:, 0:2], lhsT=ones[:], rhs=t1_row[:], start=True, stop=True)
         for c in range(4):
             part_taps(c)
 
@@ -212,7 +215,7 @@ def tile_dynamix_pa_kernel(tc, context, D, z, conv_w, conv_b, t1, out):
         def sum_frame(s):
             for k in range(4):
                 nc.tensor.matmul(
-                    bank["S"][:, s * SUM_COLUMNS:(s + 1) * SUM_COLUMNS], lhsT=c_by_place[:, s, :, k], rhs=ones[:],
+                    bank["S"][:, s * SUM_COLUMNS:(s + 1) * SUM_COLUMNS], lhsT=c_by_place[:, s, :, k], rhs=ones[:, 0:SUM_COLUMNS],
                     start=(k == 0), stop=(k == 3),
                 )
 
@@ -242,37 +245,33 @@ def tile_dynamix_pa_kernel(tc, context, D, z, conv_w, conv_b, t1, out):
                     stop=(t == 1),
                 )
 
-        new_bank("S", "c_sums", SUM_BANK)
         nc.vector.tensor_scalar(
             out=z_obs_sb[:], in0=bank["Z"][:], scalar1=1.0, scalar2=None, op0=ALU.mult, op1=ALU.add, accum_out=z_sum[:]
         )
+        nc.vector.reciprocal(out=inv_t1[:], in_=bank["t1"][:, 0:1])
+        new_bank("S", "c_sums", SUM_BANK)
         for s in ABS_FRAMES:
             nc.gpsimd.tensor_tensor(
                 out=diff[:, s - MAX_FRAMES, :], in0=c_sb[:, s, :], in1=z_obs_sb[:], op=ALU.subtract
             )
         for n in range(ROTATING - 2):
             transpose_bank(n)
-        for n in range(10):
+        for n in range(12):
             empty_bank(n)
             if n + ROTATING - 2 < len(ORDER):
                 transpose_bank(n + ROTATING - 2)
-            max_frame(n)
-            if n == 6:
-                for s in range(4):
-                    sum_frame(s)
-            elif n == 8:
-                nc.vector.reciprocal(out=inv_t1[:], in_=t1_bf[:])
+            if n < 10:
+                max_frame(n)
+            kind, j = ORDER[n]
+            for s in range(2 * j, min(2 * j + 2, MAX_FRAMES)) if kind == "C" else ():
+                sum_frame(s)
         nc.scalar.activation(out=two_inv_t1[:], in_=inv_t1[:], func=ACT.Copy, scale=2.0)
         quantize_w(0)
         quantize_w(1)
         quantize_c(0)
         max_frame(10)
-        for s in range(4, MAX_FRAMES):
-            sum_frame(s)
         for s in ABS_FRAMES:
             abs_frame(s)
-        empty_bank(10)
-        empty_bank(11)
 
         least = keep.tile([P, 1], F32)
         expd = keep.tile([P, FRAMES], F32)

from contextlib import ExitStack

import concourse.mybir as mybir
from concourse.masks import make_identity

F32 = mybir.dt.float32
BF16 = mybir.dt.bfloat16
U32 = mybir.dt.uint32
U8 = mybir.dt.uint8
FP8X4 = mybir.dt.float8_e4m3fn_x4
ALU = mybir.AluOpType
ACT = mybir.ActivationFunctionType
AX = mybir.AxisListType

P = 128
FRAMES = 16
LOADED = FRAMES + 1
CH = 512
LATENT = 1024
PAIRS = LOADED // 2
PSUM_BANKS = 8
FLOPS = 2 * FRAMES * P * CH * CH * 2 + 2 * CH * LATENT * P

MAX_FRAMES = 11
ABS_FRAMES = (12, 13, 14, 15, 11)
LOAD_ORDER = (0, 6, 1, 2, 7, 3, 4, 5, 8)
SUM_COLUMNS = 512 // MAX_FRAMES // 2 * 2
SCALAR_FRAMES = (1, 2, 3, 5, 7, 9)
VECTOR_FRAMES = tuple(s for s in range(FRAMES) if s not in SCALAR_FRAMES)
ORDER = (
    ("W", 0), ("W", 1), ("W", 2), ("W", 3), ("C", 0), ("C", 6), ("C", 1), ("C", 2), ("C", 7), ("C", 3),
    ("C", 4), ("C", 5), ("C", 8),
)
TAP_ENGINES = ("vector", "vector", "scalar", "vector")
WARM_UPS = 3
ROTATING = 6
SUM_BANK = 6
Z_BANK = 7
ENC_BANKS = (3, 4, 5, 7, 6, 0, 1, 2)


def tile_dynamix_pa_kernel(tc, context, D, z, conv_w, conv_b, t1, out):
    nc = tc.nc
    with ExitStack() as stack:
        keep = stack.enter_context(tc.tile_pool(name="keep", bufs=1))
        psum = stack.enter_context(tc.psum_pool(name="psum", bufs=1))
        stack.enter_context(tc.manual_schedule())

        ident = keep.tile([P, P], F32)
        make_identity(nc, ident[:])
        zeros = keep.tile([P, P], F32)
        nc.vector.memset(zeros[:], 0.0)
        t1_row = keep.tile([P, 2], BF16)
        nc.vector.memset(t1_row[:], 0.0)
        ones = keep.tile([P, P], BF16)
        nc.vector.memset(ones[:], 1.0)

        d_sb = keep.tile([P, 4, LATENT], BF16)
        z_sb = keep.tile([P, 4, 2, P], BF16)
        c_sb = keep.tile([P, LOADED, CH], BF16)
        w_sb = keep.tile([P, 4, 2 * CH], BF16)
        bias_bc = keep.tile([P, CH], BF16)

        def load_d(c):
            nc.sync.dma_start(out=d_sb[:, c, :], in_=D[c * P:(c + 1) * P, :])

        def load_frames(g):
            s0, s1 = 2 * g, min(2 * g + 2, LOADED)
            nc.sync.dma_start(out=c_sb[:, s0:s1, :], in_=context[s0:s1].rearrange("s b i -> b s i"))

        nc.scalar.dma_start(out=t1_row[0:1, 0:1], in_=t1.rearrange("(a b) -> a b", a=1))
        load_d(0)
        load_d(1)
        nc.sync.dma_start(out=z_sb[:], in_=z.rearrange("(u q e) b -> q u e b", u=4, e=2))
        load_d(2)
        load_d(3)
        for c in range(4):
            nc.sync.dma_start(out=w_sb[:, c, :], in_=conv_w[c * P:(c + 1) * P].rearrange("o i t -> o (i t)"))
        for g in LOAD_ORDER:
            load_frames(g)
        nc.sync.dma_start(out=bias_bc[:], in_=conv_b.partition_broadcast(P))

        bank = {}

        def new_bank(key, name, number):
            bank[key] = psum.tile([P, CH], F32, tag="bank%d" % number, name=name)
            return bank[key]

        d_t = keep.tile([P, 4 * CH], F32)
        d_t_words = d_t[:].rearrange("q (u i) -> q u i", u=4)
        d_t_halves = d_t[:].bitcast(BF16).rearrange("q (u i e) -> q u i e", u=4, e=2)

        def transpose_d(c):
            words = d_sb[:, c, :].bitcast(F32)
            for h in range(2):
                target = new_bank(("D", c, h), "d%d%d" % (c, h), (2 * c + h) % ROTATING)
                for v in range(2):
                    u = 2 * h + v
                    nc.tensor.transpose(target[:, v * P:(v + 1) * P], words[:, u * P:(u + 1) * P], ident[:])

        def copy_d(c):
            cols = slice(c * P, (c + 1) * P)
            nc.vector.tensor_copy(
                out=d_t_words[:, 0:2, cols], in_=bank["D", c, 0][:, 0:2 * P].rearrange("q (u i) -> q u i", u=2)
            )
            nc.scalar.copy(
                out=d_t_words[:, 2:4, cols], in_=bank["D", c, 1][:, 0:2 * P].rearrange("q (u i) -> q u i", u=2)
            )

        def z_obs_half(h, k0, k1):
            cols = slice(2 * h * P, 2 * (h + 1) * P)
            for k in range(k0, k1):
                nc.tensor.matmul(
                    bank["Z"][:, cols],
                    lhsT=z_sb[:, k // 2, k % 2, :],
                    rhs=d_t_halves[:, k // 2, cols, k % 2],
                    start=(k == 0),
                    stop=(k == 7),
                )

        w_taps = keep.tile([P, 4, 2, 2, 2 * P], BF16)

        def part_taps(c):
            for t in range(2):
                dst = w_taps[:, c, t, :, :].rearrange("o u (q e) -> o u q e", e=2)
                src = w_sb[:, c, :].rearrange("o (q u e t) -> o t u q e", u=2, e=2, t=2)[:, t]
                if TAP_ENGINES[c] == "scalar":
                    nc.scalar.copy(out=dst, in_=src)
                else:
                    nc.vector.tensor_copy(out=dst, in_=src)

        new_bank("Z", "z_obs", Z_BANK)
        new_bank("warm", "warm", ROTATING - 1)

        def warm_up():
            nc.tensor.matmul(bank["warm"][:, 0:P], lhsT=zeros[:], rhs=zeros[:], start=True, stop=True)

        for i in range(WARM_UPS):
            warm_up()
        transpose_d(0)
        copy_d(0)
        transpose_d(1)
        copy_d(1)
        warm_up()
        transpose_d(2)
        copy_d(2)
        z_obs_half(0, 0, 4)
        transpose_d(3)
        copy_d(3)
        z_obs_half(0, 4, 8)
        z_obs_half(1, 0, 8)
        new_bank("t1", "t1_bc", SUM_BANK)
        nc.tensor.matmul(bank["t1"][:, 0:2], lhsT=ones[:], rhs=t1_row[:], start=True, stop=True)
        for c in range(4):
            part_taps(c)

        c_grouped = keep.tile([P, LOADED * CH], BF16, align_bytes=64)
        c_codes = keep.tile([P, LOADED * P], U32, align_bytes=64)
        c_scales = keep.tile([P, LOADED * P], U8, align_bytes=64)
        w_grouped = keep.tile([P, 2, 4 * CH], BF16, align_bytes=64)
        w_codes = keep.tile([P, 2, CH], U32, align_bytes=64)
        w_scales = keep.tile([P, 2, CH], U8, align_bytes=64)
        w_grouped_words = (
            w_grouped[:].rearrange("q t k -> q (t k)").bitcast(F32).rearrange("q (t o u) -> q t o u", t=2, u=2)
        )
        c_by_place = c_grouped[:].rearrange("q (s b k) -> q s b k", s=LOADED, k=4)

        def frames_of(g):
            return min(2, LOADED - 2 * g)

        def transpose_bank(n):
            kind, j = ORDER[n]
            target = new_bank((kind, j), "%s%d" % (kind, j), (n + 2) % ROTATING)
            for v in range(4 if kind == "W" else 2 * frames_of(j)):
                u = v % 2
                if kind == "W":
                    words = w_taps[:, j, v // 2, u, :].bitcast(F32)
                else:
                    words = c_sb[:, 2 * j + v // 2, :].bitcast(F32)[:, u::2]
                nc.tensor.transpose(target[:, v * P:(v + 1) * P], words, ident[:])

        def empty_bank(n):
            kind, j = ORDER[n]
            if kind == "W":
                dst = w_grouped_words[:, :, j * P:(j + 1) * P, :]
                src = bank[kind, j][:].rearrange("q (t u o) -> q t o u", t=2, u=2)
            else:
                f = frames_of(j)
                dst = c_grouped[:, 2 * j * CH:(2 * j + f) * CH].bitcast(F32).rearrange(
                    "q (s b u) -> q s b u", s=f, u=2
                )
                src = bank[kind, j][:, 0:2 * f * P].rearrange("q (s u b) -> q s b u", s=f, u=2)
            nc.scalar.copy(out=dst, in_=src)

        z_obs_sb = keep.tile([P, CH], F32)
        diff = keep.tile([P, FRAMES - MAX_FRAMES, CH], F32)
        max_sum = keep.tile([P, MAX_FRAMES], F32)
        z_sum = keep.tile([P, 1], F32)
        linear = keep.tile([P, MAX_FRAMES], F32)
        dist = keep.tile([P, FRAMES], F32)
        unused = keep.tile([P, FRAMES, CH], BF16)
        inv_t1 = keep.tile([P, 1], F32)
        two_inv_t1 = keep.tile([P, 1], F32)

        def max_frame(s):
            nc.vector.scalar_tensor_tensor(
                out=unused[:, s, :], in0=c_sb[:, s, :], scalar=1.0, in1=bank["Z"][:], op0=ALU.mult, op1=ALU.max,
                accum_out=max_sum[:, s:s + 1],
            )

        def abs_frame(s):
            nc.scalar.activation(out=unused[:, s, :], in_=diff[:, s - MAX_FRAMES, :], func=ACT.Abs,
                                 scale=inv_t1[:], accum_out=dist[:, s:s + 1])

        def sum_frame(s):
            for k in range(4):
                nc.tensor.matmul(
                    bank["S"][:, s * SUM_COLUMNS:(s + 1) * SUM_COLUMNS], lhsT=c_by_place[:, s, :, k], rhs=ones[:, 0:SUM_COLUMNS],
                    start=(k == 0), stop=(k == 3),
                )

        def quantize_w(t):
            nc.vector.quantize_mx(
                out=w_codes[:, t, :].bitcast(FP8X4), scales=w_scales[:, t, :], in_=w_grouped[:, t, :]
            )

        def quantize_c(s0):
            s1 = min(s0 + 4, LOADED)
            nc.vector.quantize_mx(
                out=c_codes[:, s0 * P:s1 * P].bitcast(FP8X4),
                scales=c_scales[:, s0 * P:s1 * P],
                in_=c_grouped[:, s0 * CH:s1 * CH],
            )

        def enc_frame(s):
            target = new_bank(("X", s), "enc%d" % s, ENC_BANKS[s % PSUM_BANKS])
            for t in range(2):
                nc.tensor.matmul_mx(
                    out=target[:],
                    lhsT=c_codes[:, (s + t) * P:(s + t + 1) * P].bitcast(FP8X4),
                    lhsT_scale=c_scales[:, (s + t) * P:(s + t + 1) * P],
                    rhs=w_codes[:, t, :].bitcast(FP8X4),
                    rhs_scale=w_scales[:, t, :],
                    start=(t == 0),
                    stop=(t == 1),
                )

        nc.vector.tensor_scalar(
            out=z_obs_sb[:], in0=bank["Z"][:], scalar1=1.0, scalar2=None, op0=ALU.mult, op1=ALU.add, accum_out=z_sum[:]
        )
        nc.vector.reciprocal(out=inv_t1[:], in_=bank["t1"][:, 0:1])
        new_bank("S", "c_sums", SUM_BANK)
        for s in ABS_FRAMES:
            nc.gpsimd.tensor_tensor(
                out=diff[:, s - MAX_FRAMES, :], in0=c_sb[:, s, :], in1=z_obs_sb[:], op=ALU.subtract
            )
        for n in range(ROTATING - 2):
            transpose_bank(n)
        for n in range(12):
            empty_bank(n)
            if n + ROTATING - 2 < len(ORDER):
                transpose_bank(n + ROTATING - 2)
            if n < 10:
                max_frame(n)
            kind, j = ORDER[n]
            for s in range(2 * j, min(2 * j + 2, MAX_FRAMES)) if kind == "C" else ():
                sum_frame(s)
        nc.scalar.activation(out=two_inv_t1[:], in_=inv_t1[:], func=ACT.Copy, scale=2.0)
        quantize_w(0)
        quantize_w(1)
        quantize_c(0)
        max_frame(10)
        for s in ABS_FRAMES:
            abs_frame(s)

        least = keep.tile([P, 1], F32)
        expd = keep.tile([P, FRAMES], F32)
        total = keep.tile([P, 1], F32)
        inv_total = keep.tile([P, 1], F32)
        attn = keep.tile([P, FRAMES], F32)
        nc.vector.tensor_scalar(
            out=linear[:], in0=bank["S"][:, 0:MAX_FRAMES * SUM_COLUMNS:SUM_COLUMNS], scalar1=z_sum[:], scalar2=inv_t1[:], op0=ALU.add, op1=ALU.mult
        )
        quantize_c(4)
        nc.vector.scalar_tensor_tensor(
            out=dist[:, 0:MAX_FRAMES], in0=max_sum[:], scalar=two_inv_t1[:], in1=linear[:], op0=ALU.mult,
            op1=ALU.subtract,
        )
        nc.vector.tensor_reduce(out=least[:], in_=dist[:], axis=AX.X, op=ALU.min)
        nc.scalar.activation(out=expd[:], in_=dist[:], func=ACT.Exp, scale=-1.0, bias=least[:], accum_out=total[:])
        empty_bank(12)
        quantize_c(8)
        for s in range(PSUM_BANKS):
            enc_frame(s)
        nc.vector.reciprocal(out=inv_total[:], in_=total[:])
        nc.vector.tensor_scalar(out=attn[:], in0=expd[:], scalar1=inv_total[:], scalar2=None, op0=ALU.mult)
        quantize_c(12)
        quantize_c(16)

        sums = (keep.tile([P, CH], F32, name="sum_a"), keep.tile([P, CH], F32, name="sum_b"))
        sum_gpsimd = keep.tile([P, CH], F32)
        weighted = keep.tile([P, len(SCALAR_FRAMES), CH], F32)
        partial = keep.tile([P, CH], F32)
        result = keep.tile([P, CH], F32)

        STARTS = (0, 2)

        def vector_frame(k, cols):
            s = VECTOR_FRAMES[k]
            acc = sums[k % 2]
            start = weighted[:, STARTS[k], :] if k < 2 else acc
            nc.vector.scalar_tensor_tensor(
                out=acc[:, cols], in0=bank["X", s][:, cols], scalar=expd[:, s:s + 1], in1=start[:, cols],
                op0=ALU.mult, op1=ALU.add,
            )

        def scalar_frame(k):
            s = SCALAR_FRAMES[k]
            weight = expd if k in STARTS else attn
            nc.scalar.activation(out=weighted[:, k, :], in_=bank["X", s][:], func=ACT.Copy, scale=weight[:, s:s + 1])
            if k not in STARTS:
                nc.gpsimd.tensor_tensor(
                    out=sum_gpsimd[:], in0=(bias_bc[:] if k == 1 else sum_gpsimd[:]), in1=weighted[:, k, :], op=ALU.add
                )

        def over_total(dst, src, add, cols):
            nc.vector.scalar_tensor_tensor(
                out=dst[:, cols], in0=src[:, cols], scalar=inv_total[:], in1=add[:, cols], op0=ALU.mult, op1=ALU.add
            )

        whole = slice(0, CH)
        halves = (slice(0, CH // 2), slice(CH // 2, CH))
        started = PSUM_BANKS
        done = set()
        for s in (1, 0) + tuple(range(2, FRAMES - 1)):
            if s in SCALAR_FRAMES:
                scalar_frame(SCALAR_FRAMES.index(s))
            else:
                vector_frame(VECTOR_FRAMES.index(s), whole)
            done.add(s)
            while started < FRAMES and started - PSUM_BANKS in done:
                enc_frame(started)
                started += 1
        for cols in halves:
            vector_frame(len(VECTOR_FRAMES) - 1, cols)
        for cols in halves:
            over_total(partial, sums[0], sum_gpsimd, cols)
        for cols in halves:
            over_total(result, sums[1], partial, cols)
            nc.sync.dma_start(out=out[:, cols], in_=result[:, cols])
